import numpy as np
import ml_dtypes


def mxq(x, axis, fmt="e4m3"):
    dtype, down = {"e4m3": (ml_dtypes.float8_e4m3fn, 7), "e5m2": (ml_dtypes.float8_e5m2, 14)}[fmt]
    v = np.moveaxis(np.asarray(x, np.float32).astype(ml_dtypes.bfloat16).astype(np.float64), axis, -1)
    blocks = v.reshape(v.shape[:-1] + (-1, 32))
    amax = np.abs(blocks).max(-1, keepdims=True)
    byte = np.maximum(np.where(amax > 0, np.frexp(amax)[1] - 1 + 127, 0) - down, 1)
    scale = np.exp2(byte - 127.0)
    codes = (blocks / scale).astype(np.float32).astype(dtype).astype(np.float64)
    return np.moveaxis((codes * scale).reshape(v.shape), -1, axis)


WIDE = False


def mx_kscale(k):
    if not WIDE:
        return np.ones(k)
    levels = np.array([10, -10, 5, -5, 0])
    if k % 512:
        return np.exp2(np.random.permutation(np.resize(levels, k // 32))).repeat(32)
    a = np.empty((k // 512, 16))
    for p in range(k // 512):
        a[p, :8] = np.random.permutation(np.resize(levels, 8))
        for g in range(8):
            far = levels[np.abs(levels - a[p, g]) >= 10]
            a[p, g + 8] = far[np.random.randint(len(far))]
    return np.exp2(a.ravel()).repeat(32)


BF16 = ml_dtypes.bfloat16


def bf(x):
    return np.asarray(x, np.float32).astype(BF16)


def f64(x):
    return np.asarray(x).astype(np.float64)


T, H, QR, NH, DN, DR, KVR = 4096, 1024, 512, 2, 128, 64, 64
EPS = 1e-6


def rmsnorm(x, gamma):
    var = np.mean(np.square(x), axis=-1, keepdims=True)
    return x * (1.0 / np.sqrt(var + EPS)) * gamma


def apply_rope(x, cos, sin):
    x1, x2 = np.split(x, 2, axis=-1)
    rot = np.concatenate([-x2, x1], axis=-1)
    return x * cos + rot * sin


def draw0():
    s, t = mx_kscale(H), mx_kscale(QR)
    return {"token_x": bf(np.random.standard_normal((T, H)) * s),
            "wq_a": bf(np.random.standard_normal((H, QR)) / np.sqrt(H) / s[:, None]),
            "wq_b": bf(np.random.standard_normal((QR, NH * (DN + DR))) / np.sqrt(QR) / t[:, None]),
            "wkv": bf(np.random.standard_normal((H, KVR + DR)) / np.sqrt(H) / s[:, None]),
            "rope_cos": bf(np.random.uniform(-1.0, 1.0, (T, DR))),
            "rope_sin": bf(np.random.uniform(-1.0, 1.0, (T, DR))),
            "gamma_cq": bf((1.0 + 0.1 * np.random.standard_normal(QR)) * t),
            "gamma_ckv": bf(1.0 + 0.1 * np.random.standard_normal(KVR))}


def core(token_x, wq_a, wq_b, wkv, rope_cos, rope_sin, gamma_cq, gamma_ckv):
    cos, sin = f64(rope_cos), f64(rope_sin)
    xq = mxq(f64(token_x), 1, "e4m3")
    cq = rmsnorm(xq @ mxq(f64(wq_a), 0, "e4m3"), f64(gamma_cq))
    q = (mxq(cq, 1, "e4m3") @ mxq(f64(wq_b), 0, "e4m3")).reshape(T, NH, DN + DR)
    q_nope, q_rope = q[..., :DN], q[..., DN:]
    q_rope = apply_rope(q_rope, cos[:, None, :], sin[:, None, :])
    query = np.concatenate([q_nope, q_rope], axis=-1)
    kv = xq @ mxq(f64(wkv), 0, "e4m3")
    ckv = rmsnorm(kv[:, :KVR], f64(gamma_ckv))
    k_rope = apply_rope(kv[:, KVR:], cos, sin)
    return np.concatenate([query.reshape(T, -1), ckv, k_rope], axis=-1)


def e4m3fn_bytes(y):
    return np.clip(np.asarray(y, np.float64), -448.0, 448.0).astype(np.float32).astype(ml_dtypes.float8_e4m3fn).view(np.uint8)


def e4m3fn_values(b):
    return np.asarray(b, np.uint8).view(ml_dtypes.float8_e4m3fn).astype(np.float64)


def setup_inputs():
    d = draw0()
    x0 = np.asarray(d['token_x']).astype(np.float64)
    s = (np.max(np.abs(x0), axis=(0,), keepdims=True) / 448.0).astype(np.float32)
    out = {}
    for k, v in d.items():
        if k == 'token_x':
            out['token_x_bytes'] = e4m3fn_bytes(x0 / s.astype(np.float64))
            out['token_x_scale'] = s
        else:
            out[k] = v
    return out


def reference(token_x_bytes, token_x_scale, wq_a, wq_b, wkv, rope_cos, rope_sin, gamma_cq, gamma_ckv):
    return core(e4m3fn_values(token_x_bytes) * token_x_scale.astype(np.float64), wq_a, wq_b, wkv, rope_cos, rope_sin, gamma_cq, gamma_ckv)

@@ -1,0 +1,368 @@
+from contextlib import ExitStack
+
+import concourse.mybir as mybir
+from concourse.masks import make_identity
+
+T, H, QR = 4096, 1024, 512
+NH, DN, DR, KVR = 2, 128, 64, 64
+EPS = 1e-6
+OUT_W = 512
+
+FLOPS = 2 * T * (H * (QR + KVR + DR) + QR * NH * (DN + DR))
+
+P = 128
+N_TILES = T // P
+PAIRS = N_TILES // 2
+
+F32 = mybir.dt.float32
+BF16 = mybir.dt.bfloat16
+U32 = mybir.dt.uint32
+U8 = mybir.dt.uint8
+FP8 = mybir.dt.float8_e4m3fn
+FP8X4 = mybir.dt.float8_e4m3fn_x4
+MULT = mybir.AluOpType.mult
+ADD = mybir.AluOpType.add
+ACT = mybir.ActivationFunctionType
+
+
+def tile_mla_model_t_kernel(
+    tc, x_bytes, x_scale, wq_a, wq_b, wkv, rope_cos, rope_sin, gamma_cq, gamma_ckv, out
+):
+    nc = tc.nc
+    x_hbm = x_bytes.rearrange("(p i) k -> p i k", i=N_TILES)
+    cos_hbm = rope_cos.rearrange("(p i) d -> p i d", i=N_TILES)
+    sin_hbm = rope_sin.rearrange("(p i) d -> p i d", i=N_TILES)
+    out_hbm = out.rearrange("(p i) c -> p i c", i=N_TILES)
+
+    with ExitStack() as ctx:
+        keep = ctx.enter_context(tc.tile_pool(name="keep", bufs=1))
+        work = ctx.enter_context(tc.tile_pool(name="work", bufs=2))
+        ps_x = ctx.enter_context(tc.psum_pool(name="ps_x", bufs=2))
+        ps_a = ctx.enter_context(tc.psum_pool(name="ps_a", bufs=2))
+        ps_c = ctx.enter_context(tc.psum_pool(name="ps_c", bufs=1))
+        ps_q = ctx.enter_context(tc.psum_pool(name="ps_q", bufs=3))
+        ctx.enter_context(tc.manual_schedule())
+
+        xb = keep.tile([P, N_TILES * H], U8, name="xb")
+        scale = keep.tile([P, H], F32, name="scale")
+        wa_raw = keep.tile([P, 2, 4, QR], BF16, name="wa_raw")
+        wkv_raw = keep.tile([P, 2, 4, KVR + DR], BF16, name="wkv_raw")
+        wb_raw = keep.tile([P, 4, NH * (DN + DR)], BF16, name="wb_raw")
+        gq_raw = keep.tile([P, QR], BF16, name="gq_raw")
+        gq = keep.tile([P, QR], BF16, name="gq")
+        gkv = keep.tile([P, KVR], BF16, name="gkv")
+        cos = keep.tile([P, N_TILES, DR], BF16, name="cos")
+        sin = keep.tile([P, N_TILES, DR], BF16, name="sin")
+        ident = keep.tile([P, P], F32, name="ident")
+        eps = keep.tile([P, 1], F32, name="eps")
+        warm = keep.tile([P, 1], F32, name="warm")
+
+        wa_g = keep.tile([P, 2 * QR * 4], BF16, name="wa_g", align_bytes=64)
+        wa_c = keep.tile([P, 2, QR], U32, name="wa_c", align_bytes=64)
+        wa_s = keep.tile([P, 2, QR], U8, name="wa_s", align_bytes=64)
+        wkv_g = keep.tile([P, 2 * 128 * 4], BF16, name="wkv_g", align_bytes=64)
+        wkv_c = keep.tile([P, 2, 128], U32, name="wkv_c", align_bytes=64)
+        wkv_s = keep.tile([P, 2, 128], U8, name="wkv_s", align_bytes=64)
+        wb_g = keep.tile([P, 384 * 4], BF16, name="wb_g", align_bytes=64)
+        wb_c = keep.tile([P, 384], U32, name="wb_c", align_bytes=64)
+        wb_s = keep.tile([P, 384], U8, name="wb_s", align_bytes=64)
+
+        def load_x(i0, i1):
+            nc.sync.dma_start(
+                out=xb[:, i0 * H : i1 * H],
+                in_=x_hbm[:, i0:i1, :].rearrange("p i k -> p (i k)"),
+            )
+
+        wa_hbm = wq_a.rearrange("(g p j) c -> g p j c", p=P, j=4)
+        load_x(0, 2)
+        nc.sync.dma_start(out=scale[:], in_=x_scale.rearrange("o k -> (o k)").partition_broadcast(P))
+        nc.sync.dma_start(out=wa_raw[:, 0], in_=wa_hbm[0])
+        nc.sync.dma_start(out=wa_raw[:, 1], in_=wa_hbm[1])
+        load_x(2, 4)
+        nc.sync.dma_start(out=gq_raw[:], in_=gamma_cq.partition_broadcast(P))
+        nc.sync.dma_start(out=wb_raw[:], in_=wq_b.rearrange("(p j) c -> p j c", j=4))
+        wkv_hbm = wkv.rearrange("(g p j) c -> g p j c", p=P, j=4)
+        nc.sync.dma_start(out=wkv_raw[:, 0], in_=wkv_hbm[0])
+        nc.sync.dma_start(out=wkv_raw[:, 1], in_=wkv_hbm[1])
+        nc.sync.dma_start(out=sin[:], in_=sin_hbm)
+        nc.sync.dma_start(out=cos[:], in_=cos_hbm)
+        nc.sync.dma_start(out=gkv[:], in_=gamma_ckv.partition_broadcast(P))
+        for i0 in range(4, N_TILES, 4):
+            load_x(i0, i0 + 4)
+
+        make_identity(nc, ident[:])
+        nc.vector.memset(eps[:], EPS)
+        nc.vector.memset(warm[:], 1.0)
+        nc.scalar.activation(warm[:], warm[:], ACT.Sqrt)
+
+        state = {}
+
+        def wa_copy(engine, g, u):
+            dst = wa_g[:].rearrange("p (g u m e j) -> p g u m e j", g=2, u=2, e=2, j=4)[:, g, u]
+            src = wa_raw[:, g].rearrange("p j (m u e) -> p u m e j", u=2, e=2)[:, u]
+            engine(out=dst, in_=src)
+
+        def wa_quant(g):
+            nc.vector.quantize_mx(
+                out=wa_c[:, g, :].bitcast(FP8X4), scales=wa_s[:, g, :], in_=wa_g[:, g * 2048 : (g + 1) * 2048]
+            )
+
+        def wb_copies(engine):
+            dst = wb_g[:, 0:1024].rearrange("p (h c j) -> p h c j", h=2, j=4)
+            src = wb_raw[:].rearrange("p j (h c) -> p h c j", h=2)
+            engine(out=dst, in_=src[:, :, 0:DN, :])
+            dst = wb_g[:, 1024:1536].rearrange("p (h c j) -> p h c j", h=2, j=4)
+            engine(out=dst, in_=src[:, :, DN : DN + DR, :])
+            dst = wkv_g[:].rearrange("p (g h c j) -> p g h c j", g=2, h=2, j=4)
+            src = wkv_raw[:].rearrange("p g j (h c) -> p g h c j", h=2)
+            for h in range(2):
+                engine(out=dst[:, :, h], in_=src[:, :, 1 - h])
+
+        def wb_quants():
+            nc.vector.quantize_mx(
+                out=wkv_c[:].rearrange("p g c -> p (g c)").bitcast(FP8X4),
+                scales=wkv_s[:].rearrange("p g c -> p (g c)"),
+                in_=wkv_g[:],
+            )
+            nc.vector.quantize_mx(out=wb_c[:, 0:256].bitcast(FP8X4), scales=wb_s[:, 0:256], in_=wb_g[:, 0:1024])
+            nc.vector.quantize_mx(out=wb_c[:, 256:384].bitcast(FP8X4), scales=wb_s[:, 256:384], in_=wb_g[:, 1024:1536])
+
+        def mult_x(n, j):
+            xs = work.tile([P, H], BF16, name="xs", bufs=4)
+            i = 2 * n + j
+            nc.vector.tensor_tensor(out=xs[:], in0=xb[:, i * H : (i + 1) * H].bitcast(FP8), in1=scale[:], op=MULT)
+            state["xs", n, j] = xs
+
+        def turn_x(n):
+            for j in range(2):
+                xt = ps_x.tile([P, 4, P], F32, name="xt")
+                words = state["xs", n, j][:].bitcast(F32)
+                for g in range(2):
+                    for u in range(2):
+                        nc.tensor.transpose(
+                            xt[:, 2 * g + u, :], words[:, 256 * g + u : 256 * (g + 1) : 2], ident[:]
+                        )
+                state["xt", n, j] = xt
+
+        def empty_x(n):
+            xg = work.tile([P, 2048], BF16, name="xg", align_bytes=64)
+            view = xg[:].bitcast(F32).rearrange("p (j g n u) -> p j g n u", j=2, g=2, u=2)
+            for j in range(2):
+                nc.scalar.copy(out=view[:, j], in_=state["xt", n, j][:].rearrange("p (g u) n -> p g n u", g=2))
+            state["xg", n] = xg
+
+        def quant_x(n):
+            xc = work.tile([P, 512], U32, name="xc", bufs=3, align_bytes=64)
+            xsc = work.tile([P, 512], U8, name="xsc", bufs=3, align_bytes=64)
+            nc.vector.quantize_mx(out=xc[:].bitcast(FP8X4), scales=xsc[:], in_=state["xg", n][:])
+            state["xc", n] = (xc, xsc)
+
+        def mm_a(n):
+            xc, xsc = state["xc", n]
+            for j in range(2):
+                pa = ps_a.tile([P, QR], F32, name="pa")
+                for g in range(2):
+                    cols = slice((2 * j + g) * P, (2 * j + g + 1) * P)
+                    nc.tensor.matmul_mx(
+                        out=pa[:],
+                        lhsT=xc[:, cols].bitcast(FP8X4),
+                        lhsT_scale=xsc[:, cols],
+                        rhs=wa_c[:, g, :].bitcast(FP8X4),
+                        rhs_scale=wa_s[:, g, :],
+                        start=(g == 0),
+                        stop=(g == 1),
+                    )
+                state["pa", n, j] = pa
+
+        def square_a(n, ss):
+            for j in range(2):
+                junk = work.tile([P, QR], BF16, name="junk")
+                nc.scalar.activation(
+                    junk[:], state["pa", n, j][:], ACT.Square, scale=QR**-0.5, accum_out=ss[:, j : j + 1]
+                )
+
+        def norm_a(n, rinv):
+            cqs = [work.tile([P, QR], BF16, name="cqs0"), work.tile([P, QR], BF16, name="cqs1")]
+            for j in range(2):
+                nc.vector.scalar_tensor_tensor(
+                    out=cqs[j][:],
+                    in0=state["pa", n, j][:],
+                    scalar=rinv[:, j : j + 1],
+                    in1=gq[:],
+                    op0=MULT,
+                    op1=MULT,
+                )
+            state["cqs", n] = cqs
+
+        def turn_c(n):
+            ct = ps_c.tile([P, 2, 2, P], F32, name="ct")
+            for j in range(2):
+                words = state["cqs", n][j][:].bitcast(F32)
+                for u in range(2):
+                    nc.tensor.transpose(ct[:, j, u, :], words[:, u * P : (u + 1) * P], ident[:])
+            state["ct", n] = ct
+
+        def empty_c(n):
+            cg = work.tile([P, 1024], BF16, name="cg", align_bytes=64)
+            nc.scalar.copy(
+                out=cg[:].bitcast(F32).rearrange("p (j n u) -> p j n u", j=2, u=2),
+                in_=state["ct", n][:].rearrange("p j u n -> p j n u"),
+            )
+            state["cg", n] = cg
+
+        def quant_c(n):
+            cc = work.tile([P, 256], U32, name="cc", align_bytes=64)
+            cs = work.tile([P, 256], U8, name="cs", align_bytes=64)
+            nc.vector.quantize_mx(out=cc[:].bitcast(FP8X4), scales=cs[:], in_=state["cg", n][:])
+            state["cc", n] = (cc, cs)
+
+        def mm_q(n):
+            cc, cs = state["cc", n]
+            xc, xsc = state["xc", n]
+            for j in range(2):
+                pq = ps_q.tile([P, OUT_W], F32, name="pq")
+                cols = slice(j * P, (j + 1) * P)
+                for c0, c1, o0 in ((0, 256, 0), (256, 384, 256)):
+                    nc.tensor.matmul_mx(
+                        out=pq[:, o0 : o0 + c1 - c0],
+                        lhsT=cc[:, cols].bitcast(FP8X4),
+                        lhsT_scale=cs[:, cols],
+                        rhs=wb_c[:, c0:c1].bitcast(FP8X4),
+                        rhs_scale=wb_s[:, c0:c1],
+                        start=True,
+                        stop=True,
+                    )
+                for g in range(2):
+                    xcols = slice((2 * j + g) * P, (2 * j + g + 1) * P)
+                    nc.tensor.matmul_mx(
+                        out=pq[:, 384:512],
+                        lhsT=xc[:, xcols].bitcast(FP8X4),
+                        lhsT_scale=xsc[:, xcols],
+                        rhs=wkv_c[:, g, :].bitcast(FP8X4),
+                        rhs_scale=wkv_s[:, g, :],
+                        start=(g == 0),
+                        stop=(g == 1),
+                    )
+                state["pq", n, j] = pq
+
+        def nope(n):
+            ot = work.tile([P, 2, 576], F32, name="ot", bufs=3)
+            for j in range(2):
+                pq = state["pq", n, j]
+                nc.scalar.copy(
+                    out=ot[:, j, 0:384].rearrange("p (h c) -> p h c", h=2)[:, :, 0:DN],
+                    in_=pq[:, 0:256].rearrange("p (h c) -> p h c", h=2),
+                )
+            state["ot", n] = ot
+
+        def square_kv(n, ss):
+            for j in range(2):
+                junk = work.tile([P, KVR], BF16, name="junk2")
+                nc.scalar.activation(
+                    junk[:], state["pq", n, j][:, 448:512], ACT.Square, scale=KVR**-0.5, accum_out=ss[:, 2 + j : 3 + j]
+                )
+
+        def rope(n, j):
+            if j == 0:
+                state["mt", n] = work.tile([P, 2, 2, 192], F32, name="mt")
+            mt = state["mt", n]
+            i = 2 * n + j
+            u = state["pq", n, j][:, 256:448]
+            nc.vector.tensor_tensor(
+                out=mt[:, j, 0, :].rearrange("p (s d) -> p s d", s=3),
+                in0=u.rearrange("p (s d) -> p s d", s=3),
+                in1=cos[:, i, :].unsqueeze(1).to_broadcast([P, 3, DR]),
+                op=MULT,
+            )
+            nc.vector.tensor_tensor(
+                out=mt[:, j, 1, :].rearrange("p (s h d) -> p s h d", s=3, h=2),
+                in0=u.rearrange("p (s h d) -> p s h d", s=3, h=2)[:, :, ::-1, :],
+                in1=sin[:, i, :].rearrange("p (h d) -> p h d", h=2).unsqueeze(1).to_broadcast([P, 3, 2, DR // 2]),
+                op=MULT,
+            )
+
+        def rope_add(n):
+            mt, ot = state["mt", n], state["ot", n]
+            nc.gpsimd.tensor_tensor(
+                out=ot[:].rearrange("p j (s c) -> p j s c", s=3)[:, :, :, DN : DN + DR],
+                in0=mt[:, :, 0, :].rearrange("p j (s d) -> p j s d", s=3),
+                in1=mt[:, :, 1, :].rearrange("p j (s d) -> p j s d", s=3),
+                op=ADD,
+            )
+
+        def ckv(n, rinv):
+            for j in range(2):
+                nc.vector.scalar_tensor_tensor(
+                    out=state["ot", n][:, j, 384:448],
+                    in0=state["pq", n, j][:, 448:512],
+                    scalar=rinv[:, 2 + j : 3 + j],
+                    in1=gkv[:],
+                    op0=MULT,
+                    op1=MULT,
+                )
+
+        def store(n):
+            ot = state["ot", n]
+            nc.sync.dma_start(out=out_hbm[:, 2 * n : 2 * n + 2, 0:448], in_=ot[:, :, 0:448])
+            nc.sync.dma_start(out=out_hbm[:, 2 * n : 2 * n + 2, 448:512], in_=ot[:, :, 512:576])
+
+        for s in range(PAIRS + 2):
+            x_new, mid, old = s < PAIRS, 1 <= s <= PAIRS, s >= 2
+            ss = work.tile([P, 4], F32, name="ss")
+            if s == 1:
+                wb_copies(nc.scalar.copy)
+            if mid:
+                quant_x(s - 1)
+                mm_a(s - 1)
+            if x_new:
+                mult_x(s, 0)
+            if s == 2:
+                wb_quants()
+            if old:
+                quant_c(s - 2)
+                mm_q(s - 2)
+            if x_new:
+                mult_x(s, 1)
+            if s == 0:
+                wa_copy(nc.scalar.copy, 0, 0)
+                wa_copy(nc.scalar.copy, 0, 1)
+                wa_copy(nc.vector.tensor_copy, 1, 0)
+                wa_copy(nc.vector.tensor_copy, 1, 1)
+                wa_quant(0)
+                wa_quant(1)
+                nc.vector.tensor_copy(
+                    out=gq[:].rearrange("p (u m e) -> p u m e", u=2, e=2),
+                    in_=gq_raw[:].rearrange("p (m u e) -> p u m e", u=2, e=2),
+                )
+            if s == 1:
+                nc.vector.tensor_scalar(
+                    out=sin[:, :, 0 : DR // 2], in0=sin[:, :, 0 : DR // 2], scalar1=-1.0, scalar2=None, op0=MULT
+                )
+            if mid:
+                square_a(s - 1, ss)
+            if old:
+                square_kv(s - 2, ss)
+            lo, hi = (0 if mid else 2), (4 if old else 2)
+            if mid or old:
+                std = work.tile([P, 4], F32, name="std")
+                rinv = work.tile([P, 4], F32, name="rinv")
+                nc.scalar.activation(std[:, lo:hi], ss[:, lo:hi], ACT.Sqrt, bias=eps[:])
+            if x_new:
+                turn_x(s)
+                empty_x(s)
+            if old:
+                nope(s - 2)
+            if old:
+                rope(s - 2, 0)
+            if mid or old:
+                nc.vector.reciprocal(out=rinv[:, lo:hi], in_=std[:, lo:hi])
+            if old:
+                rope(s - 2, 1)
+                rope_add(s - 2)
+            if mid:
+                norm_a(s - 1, rinv)
+                turn_c(s - 1)
+                empty_c(s - 1)
+            if old:
+                ckv(s - 2, rinv)
+                store(s - 2)

@@ -108,15 +108,10 @@ def tile_mla_model_t_kernel(
             )
 
         def wb_copies(engine):
-            dst = wb_g[:, 0:1024].rearrange("p (h c j) -> p h c j", h=2, j=4)
-            src = wb_raw[:].rearrange("p j (h c) -> p h c j", h=2)
-            engine(out=dst, in_=src[:, :, 0:DN, :])
-            dst = wb_g[:, 1024:1536].rearrange("p (h c j) -> p h c j", h=2, j=4)
-            engine(out=dst, in_=src[:, :, DN : DN + DR, :])
-            dst = wkv_g[:].rearrange("p (g h c j) -> p g h c j", g=2, h=2, j=4)
-            src = wkv_raw[:].rearrange("p g j (h c) -> p g h c j", h=2)
-            for h in range(2):
-                engine(out=dst[:, :, h], in_=src[:, :, 1 - h])
+            engine(out=wb_g[:].rearrange("p (c j) -> p c j", j=4), in_=wb_raw[:].rearrange("p j c -> p c j"))
+            engine(
+                out=wkv_g[:].rearrange("p (g c j) -> p g c j", g=2, j=4), in_=wkv_raw[:].rearrange("p g j c -> p g c j")
+            )
 
         def wb_quants():
             nc.vector.quantize_mx(
@@ -128,82 +123,84 @@ def tile_mla_model_t_kernel(
             nc.vector.quantize_mx(out=wb_c[:, 256:384].bitcast(FP8X4), scales=wb_s[:, 256:384], in_=wb_g[:, 1024:1536])
 
         def mult_x(n, j):
-            xs = work.tile([P, H], BF16, name="xs", bufs=4)
+            xs = work.tile([P, H], BF16, name="xs", bufs=6)
             i = 2 * n + j
             nc.vector.tensor_tensor(out=xs[:], in0=xb[:, i * H : (i + 1) * H].bitcast(FP8), in1=scale[:], op=MULT)
             state["xs", n, j] = xs
 
-        def turn_x(n):
-            for j in range(2):
-                xt = ps_x.tile([P, 4, P], F32, name="xt")
-                words = state["xs", n, j][:].bitcast(F32)
-                for g in range(2):
-                    for u in range(2):
-                        nc.tensor.transpose(
-                            xt[:, 2 * g + u, :], words[:, 256 * g + u : 256 * (g + 1) : 2], ident[:]
-                        )
-                state["xt", n, j] = xt
+        def turn_x(n, j):
+            xt = ps_x.tile([P, 4, P], F32, name="xt")
+            words = state["xs", n, j][:].bitcast(F32)
+            for g in range(2):
+                for u in range(2):
+                    nc.tensor.transpose(xt[:, 2 * g + u, :], words[:, 256 * g + u : 256 * (g + 1) : 2], ident[:])
+            state["xt", n, j] = xt
 
-        def empty_x(n):
-            xg = work.tile([P, 2048], BF16, name="xg", align_bytes=64)
-            view = xg[:].bitcast(F32).rearrange("p (j g n u) -> p j g n u", j=2, g=2, u=2)
-            for j in range(2):
-                nc.scalar.copy(out=view[:, j], in_=state["xt", n, j][:].rearrange("p (g u) n -> p g n u", g=2))
-            state["xg", n] = xg
+        def empty_x(n, j):
+            if j == 0:
+                state["xg", n] = work.tile([P, 2048], BF16, name="xg", bufs=3, align_bytes=64)
+            view = state["xg", n][:].bitcast(F32).rearrange("p (j g n u) -> p j g n u", j=2, g=2, u=2)
+            nc.scalar.copy(out=view[:, j], in_=state["xt", n, j][:].rearrange("p (g u) n -> p g n u", g=2))
 
         def quant_x(n):
-            xc = work.tile([P, 512], U32, name="xc", bufs=3, align_bytes=64)
-            xsc = work.tile([P, 512], U8, name="xsc", bufs=3, align_bytes=64)
+            xc = work.tile([P, 512], U32, name="xc", bufs=4, align_bytes=64)
+            xsc = work.tile([P, 512], U8, name="xsc", bufs=4, align_bytes=64)
             nc.vector.quantize_mx(out=xc[:].bitcast(FP8X4), scales=xsc[:], in_=state["xg", n][:])
             state["xc", n] = (xc, xsc)
 
-        def mm_a(n):
+        def mm_a(n, j):
             xc, xsc = state["xc", n]
-            for j in range(2):
-                pa = ps_a.tile([P, QR], F32, name="pa")
-                for g in range(2):
-                    cols = slice((2 * j + g) * P, (2 * j + g + 1) * P)
-                    nc.tensor.matmul_mx(
-                        out=pa[:],
-                        lhsT=xc[:, cols].bitcast(FP8X4),
-                        lhsT_scale=xsc[:, cols],
-                        rhs=wa_c[:, g, :].bitcast(FP8X4),
-                        rhs_scale=wa_s[:, g, :],
-                        start=(g == 0),
-                        stop=(g == 1),
-                    )
-                state["pa", n, j] = pa
-
-        def square_a(n, ss):
-            for j in range(2):
-                junk = work.tile([P, QR], BF16, name="junk")
-                nc.scalar.activation(
-                    junk[:], state["pa", n, j][:], ACT.Square, scale=QR**-0.5, accum_out=ss[:, j : j + 1]
+            pa = ps_a.tile([P, QR], F32, name="pa")
+            for g in range(2):
+                cols = slice((2 * j + g) * P, (2 * j + g + 1) * P)
+                nc.tensor.matmul_mx(
+                    out=pa[:],
+                    lhsT=xc[:, cols].bitcast(FP8X4),
+                    lhsT_scale=xsc[:, cols],
+                    rhs=wa_c[:, g, :].bitcast(FP8X4),
+                    rhs_scale=wa_s[:, g, :],
+                    start=(g == 0),
+                    stop=(g == 1),
                 )
+            state["pa", n, j] = pa
 
-        def norm_a(n, rinv):
-            cqs = [work.tile([P, QR], BF16, name="cqs0"), work.tile([P, QR], BF16, name="cqs1")]
-            for j in range(2):
-                nc.vector.scalar_tensor_tensor(
-                    out=cqs[j][:],
-                    in0=state["pa", n, j][:],
-                    scalar=rinv[:, j : j + 1],
-                    in1=gq[:],
-                    op0=MULT,
-                    op1=MULT,
-                )
-            state["cqs", n] = cqs
+        def stat(kind, s):
+            if (kind, s) not in state:
+                state[kind, s] = work.tile([P, 4], F32, name=kind, bufs=4)
+            return state[kind, s]
 
-        def turn_c(n):
-            ct = ps_c.tile([P, 2, 2, P], F32, name="ct")
-            for j in range(2):
-                words = state["cqs", n][j][:].bitcast(F32)
-                for u in range(2):
-                    nc.tensor.transpose(ct[:, j, u, :], words[:, u * P : (u + 1) * P], ident[:])
-            state["ct", n] = ct
+        def square_a(n, j):
+            junk = work.tile([P, QR], BF16, name="junk")
+            ss = stat("ss", n + LAG["rec"])
+            nc.scalar.activation(junk[:], state["pa", n, j][:], ACT.Square, scale=QR**-0.5, accum_out=ss[:, j : j + 1])
+
+        def sqrt(s, lo, hi):
+            nc.scalar.activation(stat("std", s)[:, lo:hi], stat("ss", s)[:, lo:hi], ACT.Sqrt, bias=eps[:])
+
+        def recip(s, lo, hi):
+            nc.vector.reciprocal(out=stat("rinv", s)[:, lo:hi], in_=stat("std", s)[:, lo:hi])
+
+        def norm_a(n, j):
+            cqs = work.tile([P, QR], BF16, name="cqs", bufs=4)
+            nc.vector.scalar_tensor_tensor(
+                out=cqs[:],
+                in0=state["pa", n, j][:],
+                scalar=stat("rinv", n + LAG["rec"])[:, j : j + 1],
+                in1=gq[:],
+                op0=MULT,
+                op1=MULT,
+            )
+            state["cqs", n, j] = cqs
+
+        def turn_c(n, j):
+            if j == 0:
+                state["ct", n] = ps_c.tile([P, 2, 2, P], F32, name="ct")
+            words = state["cqs", n, j][:].bitcast(F32)
+            for u in range(2):
+                nc.tensor.transpose(state["ct", n][:, j, u, :], words[:, u * P : (u + 1) * P], ident[:])
 
         def empty_c(n):
-            cg = work.tile([P, 1024], BF16, name="cg", align_bytes=64)
+            cg = work.tile([P, 1024], BF16, name="cg", bufs=3, align_bytes=64)
             nc.scalar.copy(
                 out=cg[:].bitcast(F32).rearrange("p (j n u) -> p j n u", j=2, u=2),
                 in_=state["ct", n][:].rearrange("p j u n -> p j n u"),
@@ -211,158 +208,172 @@ def tile_mla_model_t_kernel(
             state["cg", n] = cg
 
         def quant_c(n):
-            cc = work.tile([P, 256], U32, name="cc", align_bytes=64)
-            cs = work.tile([P, 256], U8, name="cs", align_bytes=64)
+            cc = work.tile([P, 256], U32, name="cc", bufs=3, align_bytes=64)
+            cs = work.tile([P, 256], U8, name="cs", bufs=3, align_bytes=64)
             nc.vector.quantize_mx(out=cc[:].bitcast(FP8X4), scales=cs[:], in_=state["cg", n][:])
             state["cc", n] = (cc, cs)
 
-        def mm_q(n):
+        def mm_q(n, j):
             cc, cs = state["cc", n]
             xc, xsc = state["xc", n]
-            for j in range(2):
-                pq = ps_q.tile([P, OUT_W], F32, name="pq")
-                cols = slice(j * P, (j + 1) * P)
-                for c0, c1, o0 in ((0, 256, 0), (256, 384, 256)):
-                    nc.tensor.matmul_mx(
-                        out=pq[:, o0 : o0 + c1 - c0],
-                        lhsT=cc[:, cols].bitcast(FP8X4),
-                        lhsT_scale=cs[:, cols],
-                        rhs=wb_c[:, c0:c1].bitcast(FP8X4),
-                        rhs_scale=wb_s[:, c0:c1],
-                        start=True,
-                        stop=True,
-                    )
-                for g in range(2):
-                    xcols = slice((2 * j + g) * P, (2 * j + g + 1) * P)
-                    nc.tensor.matmul_mx(
-                        out=pq[:, 384:512],
-                        lhsT=xc[:, xcols].bitcast(FP8X4),
-                        lhsT_scale=xsc[:, xcols],
-                        rhs=wkv_c[:, g, :].bitcast(FP8X4),
-                        rhs_scale=wkv_s[:, g, :],
-                        start=(g == 0),
-                        stop=(g == 1),
-                    )
-                state["pq", n, j] = pq
-
-        def nope(n):
-            ot = work.tile([P, 2, 576], F32, name="ot", bufs=3)
-            for j in range(2):
-                pq = state["pq", n, j]
-                nc.scalar.copy(
-                    out=ot[:, j, 0:384].rearrange("p (h c) -> p h c", h=2)[:, :, 0:DN],
-                    in_=pq[:, 0:256].rearrange("p (h c) -> p h c", h=2),
+            pq = ps_q.tile([P, OUT_W], F32, name="pq")
+            cols = slice(j * P, (j + 1) * P)
+            for c0, c1 in ((0, 256), (256, 384)):
+                nc.tensor.matmul_mx(
+                    out=pq[:, 128 + c0 : 128 + c1],
+                    lhsT=cc[:, cols].bitcast(FP8X4),
+                    lhsT_scale=cs[:, cols],
+                    rhs=wb_c[:, c0:c1].bitcast(FP8X4),
+                    rhs_scale=wb_s[:, c0:c1],
+                    start=True,
+                    stop=True,
                 )
-            state["ot", n] = ot
-
-        def square_kv(n, ss):
-            for j in range(2):
-                junk = work.tile([P, KVR], BF16, name="junk2")
-                nc.scalar.activation(
-                    junk[:], state["pq", n, j][:, 448:512], ACT.Square, scale=KVR**-0.5, accum_out=ss[:, 2 + j : 3 + j]
+            for g in range(2):
+                xcols = slice((2 * j + g) * P, (2 * j + g + 1) * P)
+                nc.tensor.matmul_mx(
+                    out=pq[:, 0:128],
+                    lhsT=xc[:, xcols].bitcast(FP8X4),
+                    lhsT_scale=xsc[:, xcols],
+                    rhs=wkv_c[:, g, :].bitcast(FP8X4),
+                    rhs_scale=wkv_s[:, g, :],
+                    start=(g == 0),
+                    stop=(g == 1),
                 )
+            state["pq", n, j] = pq
+
+        def out_tile(n):
+            if ("ot", n) not in state:
+                state["ot", n] = work.tile([P, 2, OUT_W], F32, name="ot", bufs=5)
+                state["raw", n] = work.tile([P, 2, KVR], F32, name="raw", bufs=4)
+            return state["ot", n]
+
+        def copy_q(n, j):
+            ot = out_tile(n)
+            pq = state["pq", n, j]
+            nc.scalar.copy(
+                out=ot[:, j, 128:512].rearrange("p (h c) -> p h c", h=2)[:, :, 0:DN],
+                in_=pq[:, 128:512].rearrange("p (h c) -> p h c", h=2)[:, :, 0:DN],
+            )
+            nc.scalar.copy(out=state["raw", n][:, j, :], in_=pq[:, 0:KVR])
+
+        def square_kv(n, j):
+            junk = work.tile([P, KVR], BF16, name="junk2")
+            ss = stat("ss", n + LAG["ckv"])
+            nc.scalar.activation(
+                junk[:], state["raw", n][:, j, :], ACT.Square, scale=KVR**-0.5, accum_out=ss[:, 2 + j : 3 + j]
+            )
 
         def rope(n, j):
             if j == 0:
-                state["mt", n] = work.tile([P, 2, 2, 192], F32, name="mt")
+                state["mt", n] = work.tile([P, 2, 2, 192], F32, name="mt", bufs=3)
             mt = state["mt", n]
             i = 2 * n + j
-            u = state["pq", n, j][:, 256:448]
+            u = state["pq", n, j][:].rearrange("p (b d) -> p b d", d=64)[:, 1:8:3, :]
             nc.vector.tensor_tensor(
                 out=mt[:, j, 0, :].rearrange("p (s d) -> p s d", s=3),
-                in0=u.rearrange("p (s d) -> p s d", s=3),
+                in0=u,
                 in1=cos[:, i, :].unsqueeze(1).to_broadcast([P, 3, DR]),
                 op=MULT,
             )
             nc.vector.tensor_tensor(
                 out=mt[:, j, 1, :].rearrange("p (s h d) -> p s h d", s=3, h=2),
-                in0=u.rearrange("p (s h d) -> p s h d", s=3, h=2)[:, :, ::-1, :],
+                in0=u.rearrange("p s (h d) -> p s h d", h=2)[:, :, ::-1, :],
                 in1=sin[:, i, :].rearrange("p (h d) -> p h d", h=2).unsqueeze(1).to_broadcast([P, 3, 2, DR // 2]),
                 op=MULT,
             )
 
-        def rope_add(n):
-            mt, ot = state["mt", n], state["ot", n]
-            nc.gpsimd.tensor_tensor(
-                out=ot[:].rearrange("p j (s c) -> p j s c", s=3)[:, :, :, DN : DN + DR],
-                in0=mt[:, :, 0, :].rearrange("p j (s d) -> p j s d", s=3),
-                in1=mt[:, :, 1, :].rearrange("p j (s d) -> p j s d", s=3),
+        def rope_add(n, j0, j1, engine):
+            mt, ot = state["mt", n], out_tile(n)
+            engine.tensor_tensor(
+                out=ot[:, j0:j1].rearrange("p j (b d) -> p j b d", d=64)[:, :, 1:8:3, :],
+                in0=mt[:, j0:j1, 0, :].rearrange("p j (s d) -> p j s d", s=3),
+                in1=mt[:, j0:j1, 1, :].rearrange("p j (s d) -> p j s d", s=3),
                 op=ADD,
             )
 
-        def ckv(n, rinv):
-            for j in range(2):
-                nc.vector.scalar_tensor_tensor(
-                    out=state["ot", n][:, j, 384:448],
-                    in0=state["pq", n, j][:, 448:512],
-                    scalar=rinv[:, 2 + j : 3 + j],
-                    in1=gkv[:],
-                    op0=MULT,
-                    op1=MULT,
-                )
+        def ckv(n, j):
+            nc.vector.scalar_tensor_tensor(
+                out=state["ot", n][:, j, 0:KVR],
+                in0=state["raw", n][:, j, :],
+                scalar=stat("rinv", n + LAG["ckv"])[:, 2 + j : 3 + j],
+                in1=gkv[:],
+                op0=MULT,
+                op1=MULT,
+            )
 
         def store(n):
             ot = state["ot", n]
-            nc.sync.dma_start(out=out_hbm[:, 2 * n : 2 * n + 2, 0:448], in_=ot[:, :, 0:448])
-            nc.sync.dma_start(out=out_hbm[:, 2 * n : 2 * n + 2, 448:512], in_=ot[:, :, 512:576])
+            nc.sync.dma_start(out=out_hbm[:, 2 * n : 2 * n + 2, 0:384], in_=ot[:, :, 128:512])
+            nc.sync.dma_start(out=out_hbm[:, 2 * n : 2 * n + 2, 384:512], in_=ot[:, :, 0:128])
 
-        for s in range(PAIRS + 2):
-            x_new, mid, old = s < PAIRS, 1 <= s <= PAIRS, s >= 2
-            ss = work.tile([P, 4], F32, name="ss")
-            if s == 1:
-                wb_copies(nc.scalar.copy)
-            if mid:
-                quant_x(s - 1)
-                mm_a(s - 1)
-            if x_new:
-                mult_x(s, 0)
-            if s == 2:
-                wb_quants()
-            if old:
-                quant_c(s - 2)
-                mm_q(s - 2)
-            if x_new:
-                mult_x(s, 1)
-            if s == 0:
-                wa_copy(nc.scalar.copy, 0, 0)
-                wa_copy(nc.scalar.copy, 0, 1)
-                wa_copy(nc.vector.tensor_copy, 1, 0)
-                wa_copy(nc.vector.tensor_copy, 1, 1)
-                wa_quant(0)
-                wa_quant(1)
-                nc.vector.tensor_copy(
-                    out=gq[:].rearrange("p (u m e) -> p u m e", u=2, e=2),
-                    in_=gq_raw[:].rearrange("p (m u e) -> p u m e", u=2, e=2),
-                )
-            if s == 1:
-                nc.vector.tensor_scalar(
-                    out=sin[:, :, 0 : DR // 2], in0=sin[:, :, 0 : DR // 2], scalar1=-1.0, scalar2=None, op0=MULT
-                )
-            if mid:
-                square_a(s - 1, ss)
-            if old:
-                square_kv(s - 2, ss)
-            lo, hi = (0 if mid else 2), (4 if old else 2)
-            if mid or old:
-                std = work.tile([P, 4], F32, name="std")
-                rinv = work.tile([P, 4], F32, name="rinv")
-                nc.scalar.activation(std[:, lo:hi], ss[:, lo:hi], ACT.Sqrt, bias=eps[:])
-            if x_new:
-                turn_x(s)
-                empty_x(s)
-            if old:
-                nope(s - 2)
-            if old:
-                rope(s - 2, 0)
-            if mid or old:
-                nc.vector.reciprocal(out=rinv[:, lo:hi], in_=std[:, lo:hi])
-            if old:
-                rope(s - 2, 1)
-                rope_add(s - 2)
-            if mid:
-                norm_a(s - 1, rinv)
-                turn_c(s - 1)
-                empty_c(s - 1)
-            if old:
-                ckv(s - 2, rinv)
-                store(s - 2)
+        def first():
+            wa_copy(nc.scalar.copy, 0, 0)
+            wa_copy(nc.scalar.copy, 0, 1)
+            wa_copy(nc.vector.tensor_copy, 1, 0)
+            wa_copy(nc.vector.tensor_copy, 1, 1)
+            wa_quant(0)
+            wa_quant(1)
+            nc.vector.tensor_copy(
+                out=gq[:].rearrange("p (u m e) -> p u m e", u=2, e=2),
+                in_=gq_raw[:].rearrange("p (m u e) -> p u m e", u=2, e=2),
+            )
+
+        def negate_sin():
+            nc.vector.tensor_scalar(
+                out=sin[:, :, 0 : DR // 2], in0=sin[:, :, 0 : DR // 2], scalar1=-1.0, scalar2=None, op0=MULT
+            )
+
+        LAG = dict(M=0, QX=1, rec=1, QC=2, R=3, cp=3, ckv=4)
+        ORDER = "QX R0 mmA0 mmA1 M0 sqA0 TX0 M1 sqA1 R1 TX1 QC sqrt mmQ0 EX0 cpQ0 rec mmQ1 add EX1 N0 N1 TC0 TC1 K cpQ1 sqK store EC".split()
+        OPS = dict(
+            M0=("M", lambda n: mult_x(n, 0)),
+            M1=("M", lambda n: mult_x(n, 1)),
+            TX0=("M", lambda n: turn_x(n, 0)),
+            TX1=("M", lambda n: turn_x(n, 1)),
+            EX0=("M", lambda n: empty_x(n, 0)),
+            EX1=("M", lambda n: empty_x(n, 1)),
+            QX=("QX", quant_x),
+            mmA0=("QX", lambda n: mm_a(n, 0)),
+            mmA1=("QX", lambda n: mm_a(n, 1)),
+            sqA0=("QX", lambda n: square_a(n, 0)),
+            sqA1=("QX", lambda n: square_a(n, 1)),
+            N0=("rec", lambda n: norm_a(n, 0)),
+            N1=("rec", lambda n: norm_a(n, 1)),
+            TC0=("rec", lambda n: turn_c(n, 0)),
+            TC1=("rec", lambda n: turn_c(n, 1)),
+            EC=("rec", empty_c),
+            QC=("QC", quant_c),
+            mmQ0=("QC", lambda n: mm_q(n, 0)),
+            mmQ1=("QC", lambda n: mm_q(n, 1)),
+            R0=("R", lambda n: rope(n, 0)),
+            R1=("R", lambda n: rope(n, 1)),
+            add0=("R", lambda n: rope_add(n, 0, 1, ADD_ENG)),
+            add1=("R", lambda n: rope_add(n, 1, 2, ADD_ENG)),
+            add=("R", lambda n: rope_add(n, 0, 2, ADD_ENG)),
+            cpQ0=("cp", lambda n: copy_q(n, 0)),
+            cpQ1=("cp", lambda n: copy_q(n, 1)),
+            sqK=("cp", lambda n: (square_kv(n, 0), square_kv(n, 1))),
+            K=("ckv", lambda n: (ckv(n, 0), ckv(n, 1))),
+            store=("ckv", store),
+        )
+        ADD_ENG = nc.vector
+        for s in range(PAIRS + LAG["ckv"]):
+            has_a, has_k = 0 <= s - LAG["rec"] < PAIRS, 0 <= s - LAG["ckv"] < PAIRS
+            lo, hi = (0 if has_a else 2), (4 if has_k else 2)
+            for op in ORDER:
+                if op in ("sqrt", "rec"):
+                    if has_a or has_k:
+                        (sqrt if op == "sqrt" else recip)(s, lo, hi)
+                    continue
+                lag = LAG[OPS[op][0]]
+                fn = OPS[op][1]
+                if op == "QC" and s == LAG["QC"]:
+                    wb_quants()
+                if 0 <= s - lag < PAIRS:
+                    fn(s - lag)
+                if s == 0 and op == "M1":
+                    first()
+                if s == 1 and op == "M0":
+                    wb_copies(nc.scalar.copy)
+                if s == 1 and op == "M1":
+                    negate_sin()

@@ -40,11 +40,12 @@ def tile_mla_model_t_kernel(
         ps_x = ctx.enter_context(tc.psum_pool(name="ps_x", bufs=2))
         ps_a = ctx.enter_context(tc.psum_pool(name="ps_a", bufs=2))
         ps_c = ctx.enter_context(tc.psum_pool(name="ps_c", bufs=1))
-        ps_q = ctx.enter_context(tc.psum_pool(name="ps_q", bufs=3))
+        ps_q = ctx.enter_context(tc.psum_pool(name="ps_q", bufs=1))
         ctx.enter_context(tc.manual_schedule())
 
         xb = keep.tile([P, N_TILES * H], U8, name="xb")
-        scale = keep.tile([P, H], F32, name="scale")
+        scale8 = keep.tile([P, 2, 4], F32, name="scale8")
+        scale = keep.tile([P, 2, H], F32, name="scale")
         wa_raw = keep.tile([P, 2, 4, QR], BF16, name="wa_raw")
         wkv_raw = keep.tile([P, 2, 4, KVR + DR], BF16, name="wkv_raw")
         wb_raw = keep.tile([P, 4, NH * (DN + DR)], BF16, name="wb_raw")
@@ -53,16 +54,18 @@ def tile_mla_model_t_kernel(
         gkv = keep.tile([P, KVR], BF16, name="gkv")
         cos = keep.tile([P, N_TILES, DR], BF16, name="cos")
         sin = keep.tile([P, N_TILES, DR], BF16, name="sin")
+        tab = keep.tile([P, N_TILES, 2, 2, DR // 2], BF16, name="tab")
         ident = keep.tile([P, P], F32, name="ident")
         eps = keep.tile([P, 1], F32, name="eps")
+        zero = keep.tile([P, 512], BF16, name="zero")
         warm = keep.tile([P, 1], F32, name="warm")
 
         wa_g = keep.tile([P, 2 * QR * 4], BF16, name="wa_g", align_bytes=64)
         wa_c = keep.tile([P, 2, QR], U32, name="wa_c", align_bytes=64)
         wa_s = keep.tile([P, 2, QR], U8, name="wa_s", align_bytes=64)
-        wkv_g = keep.tile([P, 2 * 128 * 4], BF16, name="wkv_g", align_bytes=64)
-        wkv_c = keep.tile([P, 2, 128], U32, name="wkv_c", align_bytes=64)
-        wkv_s = keep.tile([P, 2, 128], U8, name="wkv_s", align_bytes=64)
+        wkv_g = keep.tile([P, 4 * 128 * 4], BF16, name="wkv_g", align_bytes=64)
+        wkv_c = keep.tile([P, 2, 2, 128], U32, name="wkv_c", align_bytes=64)
+        wkv_s = keep.tile([P, 2, 2, 128], U8, name="wkv_s", align_bytes=64)
         wb_g = keep.tile([P, 384 * 4], BF16, name="wb_g", align_bytes=64)
         wb_c = keep.tile([P, 384], U32, name="wb_c", align_bytes=64)
         wb_s = keep.tile([P, 384], U8, name="wb_s", align_bytes=64)
@@ -74,26 +77,49 @@ def tile_mla_model_t_kernel(
             )
 
         wa_hbm = wq_a.rearrange("(g p j) c -> g p j c", p=P, j=4)
-        load_x(0, 2)
-        nc.sync.dma_start(out=scale[:], in_=x_scale.rearrange("o k -> (o k)").partition_broadcast(P))
-        nc.sync.dma_start(out=wa_raw[:, 0], in_=wa_hbm[0])
-        nc.sync.dma_start(out=wa_raw[:, 1], in_=wa_hbm[1])
-        load_x(2, 4)
-        nc.sync.dma_start(out=gq_raw[:], in_=gamma_cq.partition_broadcast(P))
-        nc.sync.dma_start(out=wb_raw[:], in_=wq_b.rearrange("(p j) c -> p j c", j=4))
+        nc.sync.dma_start(out=scale8[:], in_=x_scale.rearrange("o (h n c) -> n (o h) c", h=2, c=4))
+        for piece in "x0 x2 w0 w1".split():
+            if piece == "x0":
+                load_x(0, 2)
+            elif piece == "x2":
+                load_x(2, 4)
+            else:
+                nc.sync.dma_start(out=wa_raw[:, int(piece[1])], in_=wa_hbm[int(piece[1])])
         wkv_hbm = wkv.rearrange("(g p j) c -> g p j c", p=P, j=4)
+        nc.sync.dma_start(out=wb_raw[:], in_=wq_b.rearrange("(p j) c -> p j c", j=4))
         nc.sync.dma_start(out=wkv_raw[:, 0], in_=wkv_hbm[0])
         nc.sync.dma_start(out=wkv_raw[:, 1], in_=wkv_hbm[1])
+        nc.sync.dma_start(out=gq_raw[:], in_=gamma_cq.partition_broadcast(P))
         nc.sync.dma_start(out=sin[:], in_=sin_hbm)
         nc.sync.dma_start(out=cos[:], in_=cos_hbm)
+        load_x(4, 8)
         nc.sync.dma_start(out=gkv[:], in_=gamma_ckv.partition_broadcast(P))
-        for i0 in range(4, N_TILES, 4):
+        for i0 in range(8, N_TILES, 4):
             load_x(i0, i0 + 4)
 
         make_identity(nc, ident[:])
+        nc.gpsimd.memset(zero[:], 0.0)
         nc.vector.memset(eps[:], EPS)
         nc.vector.memset(warm[:], 1.0)
-        nc.scalar.activation(warm[:], warm[:], ACT.Sqrt)
+        nc.scalar.activation(warm[:], warm[:], ACT.Abs_reciprocal_sqrt)
+
+        def dummies(k):
+            bank = ps_q.tile([P, OUT_W], F32, name="pr", bufs=2)
+            for c in range(k):
+                nc.tensor.matmul(bank[:], lhsT=zero[:, 0:P], rhs=zero[:], start=True, stop=True)
+
+        dummies(4)
+        for half in range(2):
+            bank = ps_x.tile([P, 4, P], F32, name="xt")
+            for c in range(4):
+                nc.tensor.transpose(
+                    bank[:, c, :], scale8[:, half, c : c + 1].to_broadcast([P, P]), ident[:]
+                )
+            for copy, j in ((nc.vector.tensor_copy, 0), (nc.scalar.copy, 1)):
+                copy(
+                    out=scale[:, j, 512 * half : 512 * (half + 1)].rearrange("p (n c) -> p n c", c=4),
+                    in_=bank[:].rearrange("p c n -> p n c"),
+                )
 
         state = {}
 
@@ -107,44 +133,65 @@ def tile_mla_model_t_kernel(
                 out=wa_c[:, g, :].bitcast(FP8X4), scales=wa_s[:, g, :], in_=wa_g[:, g * 2048 : (g + 1) * 2048]
             )
 
-        def wb_copies(engine):
-            engine(out=wb_g[:].rearrange("p (c j) -> p c j", j=4), in_=wb_raw[:].rearrange("p j c -> p c j"))
-            engine(
-                out=wkv_g[:].rearrange("p (g c j) -> p g c j", g=2, j=4), in_=wkv_raw[:].rearrange("p g j c -> p g c j")
-            )
+        def wb_copy(engine, part):
+            wb_dst = wb_g[:].rearrange("p (c j) -> p c j", j=4)
+            wb_src = wb_raw[:].rearrange("p j (h c) -> p h c j", h=2)
+            kv_dst = wkv_g[:].rearrange("p (v g c j) -> p v g c j", v=2, g=2, j=4)
+            kv_src = wkv_raw[:].rearrange("p g j c -> p g c j")
+            if part == 0:
+                engine(out=wb_dst[:, 0:256].rearrange("p (h c) j -> p h c j", h=2), in_=wb_src[:, :, 0:DN])
+            elif part == 1:
+                engine(out=wb_dst[:, 256:384].rearrange("p (h c) j -> p h c j", h=2), in_=wb_src[:, :, DN:])
+            elif part == 2:
+                engine(out=kv_dst[:, 0], in_=kv_src)
+            else:
+                engine(out=kv_dst[:, 1, :, 0:64], in_=kv_src[:, :, 64:128])
+                engine(out=kv_dst[:, 1, :, 64:128], in_=kv_src[:, :, 0:64])
 
         def wb_quants():
             nc.vector.quantize_mx(
-                out=wkv_c[:].rearrange("p g c -> p (g c)").bitcast(FP8X4),
-                scales=wkv_s[:].rearrange("p g c -> p (g c)"),
+                out=wkv_c[:].rearrange("p v g c -> p (v g c)").bitcast(FP8X4),
+                scales=wkv_s[:].rearrange("p v g c -> p (v g c)"),
                 in_=wkv_g[:],
             )
             nc.vector.quantize_mx(out=wb_c[:, 0:256].bitcast(FP8X4), scales=wb_s[:, 0:256], in_=wb_g[:, 0:1024])
             nc.vector.quantize_mx(out=wb_c[:, 256:384].bitcast(FP8X4), scales=wb_s[:, 256:384], in_=wb_g[:, 1024:1536])
 
         def mult_x(n, j):
-            xs = work.tile([P, H], BF16, name="xs", bufs=6)
-            i = 2 * n + j
-            nc.vector.tensor_tensor(out=xs[:], in0=xb[:, i * H : (i + 1) * H].bitcast(FP8), in1=scale[:], op=MULT)
-            state["xs", n, j] = xs
+            if ("xs", n) not in state:
+                state["xs", n] = work.tile([P, 2 * H], BF16, name="xs", bufs=5)
+            xs = state["xs", n]
+            pieces = [(0, 2 * H)] if j is None else [(j * H, (j + 1) * H)]
+            if n == 0 and j != 1:
+                pieces = [(0, 512), (512, H)] + ([(H, 2 * H)] if j is None else [])
+            for k0, k1 in pieces:
+                nc.vector.tensor_tensor(
+                    out=xs[:, k0:k1],
+                    in0=xb[:, 2 * n * H + k0 : 2 * n * H + k1].bitcast(FP8),
+                    in1=scale[:].rearrange("p j k -> p (j k)")[:, k0 % H if n == 0 else k0 : (k1 - 1) % H + 1 if n == 0 else k1],
+                    op=MULT,
+                )
+
+        def x_grouped(n):
+            if ("xg", n) not in state:
+                state["xg", n] = work.tile([P, 2048], BF16, name="xg", bufs=4, align_bytes=64)
+            return state["xg", n]
 
         def turn_x(n, j):
             xt = ps_x.tile([P, 4, P], F32, name="xt")
-            words = state["xs", n, j][:].bitcast(F32)
+            words = state["xs", n][:, j * H : (j + 1) * H].bitcast(F32)
             for g in range(2):
                 for u in range(2):
                     nc.tensor.transpose(xt[:, 2 * g + u, :], words[:, 256 * g + u : 256 * (g + 1) : 2], ident[:])
             state["xt", n, j] = xt
 
         def empty_x(n, j):
-            if j == 0:
-                state["xg", n] = work.tile([P, 2048], BF16, name="xg", bufs=3, align_bytes=64)
-            view = state["xg", n][:].bitcast(F32).rearrange("p (j g n u) -> p j g n u", j=2, g=2, u=2)
+            view = x_grouped(n)[:].bitcast(F32).rearrange("p (j g n u) -> p j g n u", j=2, g=2, u=2)
             nc.scalar.copy(out=view[:, j], in_=state["xt", n, j][:].rearrange("p (g u) n -> p g n u", g=2))
 
         def quant_x(n):
-            xc = work.tile([P, 512], U32, name="xc", bufs=4, align_bytes=64)
-            xsc = work.tile([P, 512], U8, name="xsc", bufs=4, align_bytes=64)
+            xc = work.tile([P, 512], U32, name="xc", bufs=7, align_bytes=64)
+            xsc = work.tile([P, 512], U8, name="xsc", bufs=7, align_bytes=64)
             nc.vector.quantize_mx(out=xc[:].bitcast(FP8X4), scales=xsc[:], in_=state["xg", n][:])
             state["xc", n] = (xc, xsc)
 
@@ -166,7 +213,7 @@ def tile_mla_model_t_kernel(
 
         def stat(kind, s):
             if (kind, s) not in state:
-                state[kind, s] = work.tile([P, 4], F32, name=kind, bufs=4)
+                state[kind, s] = work.tile([P, 4], F32, name=kind, bufs=6)
             return state[kind, s]
 
         def square_a(n, j):
@@ -175,10 +222,8 @@ def tile_mla_model_t_kernel(
             nc.scalar.activation(junk[:], state["pa", n, j][:], ACT.Square, scale=QR**-0.5, accum_out=ss[:, j : j + 1])
 
         def sqrt(s, lo, hi):
-            nc.scalar.activation(stat("std", s)[:, lo:hi], stat("ss", s)[:, lo:hi], ACT.Sqrt, bias=eps[:])
+            nc.scalar.activation(stat("rinv", s)[:, lo:hi], stat("ss", s)[:, lo:hi], ACT.Abs_reciprocal_sqrt, bias=eps[:])
 
-        def recip(s, lo, hi):
-            nc.vector.reciprocal(out=stat("rinv", s)[:, lo:hi], in_=stat("std", s)[:, lo:hi])
 
         def norm_a(n, j):
             cqs = work.tile([P, QR], BF16, name="cqs", bufs=4)
@@ -200,7 +245,7 @@ def tile_mla_model_t_kernel(
                 nc.tensor.transpose(state["ct", n][:, j, u, :], words[:, u * P : (u + 1) * P], ident[:])
 
         def empty_c(n):
-            cg = work.tile([P, 1024], BF16, name="cg", bufs=3, align_bytes=64)
+            cg = work.tile([P, 1024], BF16, name="cg", bufs=4, align_bytes=64)
             nc.scalar.copy(
                 out=cg[:].bitcast(F32).rearrange("p (j n u) -> p j n u", j=2, u=2),
                 in_=state["ct", n][:].rearrange("p j u n -> p j n u"),
@@ -208,172 +253,224 @@ def tile_mla_model_t_kernel(
             state["cg", n] = cg
 
         def quant_c(n):
-            cc = work.tile([P, 256], U32, name="cc", bufs=3, align_bytes=64)
-            cs = work.tile([P, 256], U8, name="cs", bufs=3, align_bytes=64)
+            cc = work.tile([P, 256], U32, name="cc", bufs=4, align_bytes=64)
+            cs = work.tile([P, 256], U8, name="cs", bufs=4, align_bytes=64)
             nc.vector.quantize_mx(out=cc[:].bitcast(FP8X4), scales=cs[:], in_=state["cg", n][:])
             state["cc", n] = (cc, cs)
 
-        def mm_q(n, j):
+        def mm_r(n):
             cc, cs = state["cc", n]
             xc, xsc = state["xc", n]
-            pq = ps_q.tile([P, OUT_W], F32, name="pq")
-            cols = slice(j * P, (j + 1) * P)
-            for c0, c1 in ((0, 256), (256, 384)):
+            pr = ps_q.tile([P, OUT_W], F32, name="pr", bufs=2)
+            for j in range(2):
+                cols = slice(j * P, (j + 1) * P)
+                for g in range(2):
+                    xcols = slice((2 * j + g) * P, (2 * j + g + 1) * P)
+                    nc.tensor.matmul_mx(
+                        out=pr[:, 384 * j : 384 * j + 128],
+                        lhsT=xc[:, xcols].bitcast(FP8X4),
+                        lhsT_scale=xsc[:, xcols],
+                        rhs=wkv_c[:, j, g, :].bitcast(FP8X4),
+                        rhs_scale=wkv_s[:, j, g, :],
+                        start=(g == 0),
+                        stop=(g == 1),
+                    )
                 nc.tensor.matmul_mx(
-                    out=pq[:, 128 + c0 : 128 + c1],
+                    out=pr[:, 128 + 128 * j : 256 + 128 * j],
                     lhsT=cc[:, cols].bitcast(FP8X4),
                     lhsT_scale=cs[:, cols],
-                    rhs=wb_c[:, c0:c1].bitcast(FP8X4),
-                    rhs_scale=wb_s[:, c0:c1],
+                    rhs=wb_c[:, 256:384].bitcast(FP8X4),
+                    rhs_scale=wb_s[:, 256:384],
                     start=True,
                     stop=True,
                 )
-            for g in range(2):
-                xcols = slice((2 * j + g) * P, (2 * j + g + 1) * P)
+            state["pr", n] = pr
+
+        def mm_n(n):
+            cc, cs = state["cc", n]
+            pn = ps_q.tile([P, 2, 256], F32, name="pn", bufs=1)
+            for j in range(2):
+                cols = slice(j * P, (j + 1) * P)
                 nc.tensor.matmul_mx(
-                    out=pq[:, 0:128],
-                    lhsT=xc[:, xcols].bitcast(FP8X4),
-                    lhsT_scale=xsc[:, xcols],
-                    rhs=wkv_c[:, g, :].bitcast(FP8X4),
-                    rhs_scale=wkv_s[:, g, :],
-                    start=(g == 0),
-                    stop=(g == 1),
+                    out=pn[:, j, :],
+                    lhsT=cc[:, cols].bitcast(FP8X4),
+                    lhsT_scale=cs[:, cols],
+                    rhs=wb_c[:, 0:256].bitcast(FP8X4),
+                    rhs_scale=wb_s[:, 0:256],
+                    start=True,
+                    stop=True,
                 )
-            state["pq", n, j] = pq
+            state["pn", n] = pn
 
         def out_tile(n):
             if ("ot", n) not in state:
-                state["ot", n] = work.tile([P, 2, OUT_W], F32, name="ot", bufs=5)
-                state["raw", n] = work.tile([P, 2, KVR], F32, name="raw", bufs=4)
+                state["ot", n] = work.tile([P, 1152], F32, name="ot", bufs=6)
             return state["ot", n]
 
-        def copy_q(n, j):
-            ot = out_tile(n)
-            pq = state["pq", n, j]
+        def copy_n(n):
             nc.scalar.copy(
-                out=ot[:, j, 128:512].rearrange("p (h c) -> p h c", h=2)[:, :, 0:DN],
-                in_=pq[:, 128:512].rearrange("p (h c) -> p h c", h=2)[:, :, 0:DN],
+                out=out_tile(n)[:, 128:896].rearrange("p (h c) -> p h c", c=192)[:, :, 0:DN],
+                in_=state["pn", n][:].rearrange("p j (h c) -> p (j h) c", h=2),
             )
-            nc.scalar.copy(out=state["raw", n][:, j, :], in_=pq[:, 0:KVR])
 
-        def square_kv(n, j):
-            junk = work.tile([P, KVR], BF16, name="junk2")
+        def ckv_cols(tile, stride, n):
+            return tile[:, 0 : 2 * stride].rearrange("p (j c) -> p j c", j=2)[:, :, 0:n]
+
+        def square_kv(n):
             ss = stat("ss", n + LAG["ckv"])
-            nc.scalar.activation(
-                junk[:], state["raw", n][:, j, :], ACT.Square, scale=KVR**-0.5, accum_out=ss[:, 2 + j : 3 + j]
-            )
+            for j in range(2):
+                junk = work.tile([P, KVR], BF16, name="junk2")
+                nc.scalar.activation(
+                    junk[:], state["pr", n][:, 448 * j : 448 * j + 64], ACT.Square, scale=KVR**-0.5, accum_out=ss[:, 2 + j : 3 + j]
+                )
 
-        def rope(n, j):
-            if j == 0:
-                state["mt", n] = work.tile([P, 2, 2, 192], F32, name="mt", bufs=3)
-            mt = state["mt", n]
-            i = 2 * n + j
-            u = state["pq", n, j][:].rearrange("p (b d) -> p b d", d=64)[:, 1:8:3, :]
+        def gain_kv(n):
+            gv = work.tile([P, 2, KVR], F32, name="gv", bufs=5)
             nc.vector.tensor_tensor(
-                out=mt[:, j, 0, :].rearrange("p (s d) -> p s d", s=3),
-                in0=u,
-                in1=cos[:, i, :].unsqueeze(1).to_broadcast([P, 3, DR]),
+                out=gv[:],
+                in0=state["pr", n][:].rearrange("p (b c) -> p b c", c=64)[:, 0:8:7, :],
+                in1=gkv[:].unsqueeze(1).to_broadcast([P, 2, KVR]),
                 op=MULT,
             )
+            state["gv", n] = gv
+
+        def rope(n):
+            mt = work.tile([P, 6, 2, 2, 32], F32, name="mt", bufs=4)
             nc.vector.tensor_tensor(
-                out=mt[:, j, 1, :].rearrange("p (s h d) -> p s h d", s=3, h=2),
-                in0=u.rearrange("p s (h d) -> p s h d", h=2)[:, :, ::-1, :],
-                in1=sin[:, i, :].rearrange("p (h d) -> p h d", h=2).unsqueeze(1).to_broadcast([P, 3, 2, DR // 2]),
+                out=mt[:].rearrange("p (j s) h w d -> p j s h w d", j=2),
+                in0=state["pr", n][:, 64:448]
+                .rearrange("p (j s h d) -> p j s h d", j=2, s=3, h=2)
+                .unsqueeze(4)
+                .to_broadcast([P, 2, 3, 2, 2, 32]),
+                in1=tab[:, 2 * n : 2 * n + 2].unsqueeze(2).to_broadcast([P, 2, 3, 2, 2, 32]),
                 op=MULT,
             )
+            state["mt", n] = mt
 
-        def rope_add(n, j0, j1, engine):
-            mt, ot = state["mt", n], out_tile(n)
+        def token(n):
+            if 0 < n < PAIRS:
+                tok = work.tile([P, 1], BF16, name="tok")
+                nc.gpsimd.tensor_copy(out=tok[:], in_=state["xs", n][:, 0:1])
+
+        def rope_add(n, engine):
+            mt = state["mt", n][:].rearrange("p s h w d -> p s h (w d)")
             engine.tensor_tensor(
-                out=ot[:, j0:j1].rearrange("p j (b d) -> p j b d", d=64)[:, :, 1:8:3, :],
-                in0=mt[:, j0:j1, 0, :].rearrange("p j (s d) -> p j s d", s=3),
-                in1=mt[:, j0:j1, 1, :].rearrange("p j (s d) -> p j s d", s=3),
+                out=out_tile(n)[:].rearrange("p (s c) -> p s c", c=192)[:, :, 64:128],
+                in0=mt[:, :, 0, :],
+                in1=mt[:, :, 1, :],
                 op=ADD,
             )
 
-        def ckv(n, j):
-            nc.vector.scalar_tensor_tensor(
-                out=state["ot", n][:, j, 0:KVR],
-                in0=state["raw", n][:, j, :],
-                scalar=stat("rinv", n + LAG["ckv"])[:, 2 + j : 3 + j],
-                in1=gkv[:],
-                op0=MULT,
-                op1=MULT,
-            )
+        def ckv(n):
+            for j in range(2):
+                nc.scalar.activation(
+                    state["ot", n][:, 960 * j : 960 * j + 64],
+                    state["gv", n][:, j, :],
+                    ACT.Copy,
+                    scale=stat("rinv", n + LAG["ckv"])[:, 2 + j : 3 + j],
+                )
 
         def store(n):
             ot = state["ot", n]
-            nc.sync.dma_start(out=out_hbm[:, 2 * n : 2 * n + 2, 0:384], in_=ot[:, :, 128:512])
-            nc.sync.dma_start(out=out_hbm[:, 2 * n : 2 * n + 2, 384:512], in_=ot[:, :, 0:128])
+            nc.sync.dma_start(
+                out=out_hbm[:, 2 * n : 2 * n + 2, 0:384], in_=ot[:, 128:896].rearrange("p (j c) -> p j c", j=2)
+            )
+            nc.sync.dma_start(
+                out=out_hbm[:, 2 * n : 2 * n + 2, 384:512],
+                in_=ot[:].rearrange("p (b c) -> p b c", c=192)[:, 0:6:5, 0:128],
+            )
 
-        def first():
-            wa_copy(nc.scalar.copy, 0, 0)
-            wa_copy(nc.scalar.copy, 0, 1)
-            wa_copy(nc.vector.tensor_copy, 1, 0)
-            wa_copy(nc.vector.tensor_copy, 1, 1)
-            wa_quant(0)
-            wa_quant(1)
-            nc.vector.tensor_copy(
+        def prep_gq():
+            nc.scalar.copy(
                 out=gq[:].rearrange("p (u m e) -> p u m e", u=2, e=2),
                 in_=gq_raw[:].rearrange("p (m u e) -> p u m e", u=2, e=2),
             )
 
-        def negate_sin():
-            nc.vector.tensor_scalar(
-                out=sin[:, :, 0 : DR // 2], in0=sin[:, :, 0 : DR // 2], scalar1=-1.0, scalar2=None, op0=MULT
-            )
+        def tables(half):
+            if half == 0:
+                nc.scalar.copy(out=tab[:, :, 0, 1, :], in_=sin[:, :, 32:64])
+                nc.scalar.activation(tab[:, :, 1, 0, :], sin[:, :, 0:32], ACT.Copy, scale=-1.0)
+            else:
+                nc.scalar.copy(out=tab[:, :, 0, 0, :], in_=cos[:, :, 0:32])
+                nc.scalar.copy(out=tab[:, :, 1, 1, :], in_=cos[:, :, 32:64])
 
-        LAG = dict(M=0, QX=1, rec=1, QC=2, R=3, cp=3, ckv=4)
-        ORDER = "QX R0 mmA0 mmA1 M0 sqA0 TX0 M1 sqA1 R1 TX1 QC sqrt mmQ0 EX0 cpQ0 rec mmQ1 add EX1 N0 N1 TC0 TC1 K cpQ1 sqK store EC".split()
+        LAG = {'M': 0, 'X': 0, 'QX': 1, 'MA': 1, 'rec': 1, 'QC': 2, 'Q': 2, 'R': 3, 'A': 3, 'cp': 2, 'ckv': 4}
+        ORDER = "QX mmA0 mmA1 TX0 TX1 sqA0 M sqA1 sqrt R QC EX0 EX1 G mmR sqK K N0 mmN cpN TC0 N1 store add TC1 EC".split()
         OPS = dict(
-            M0=("M", lambda n: mult_x(n, 0)),
-            M1=("M", lambda n: mult_x(n, 1)),
-            TX0=("M", lambda n: turn_x(n, 0)),
-            TX1=("M", lambda n: turn_x(n, 1)),
-            EX0=("M", lambda n: empty_x(n, 0)),
-            EX1=("M", lambda n: empty_x(n, 1)),
+            M=("M", lambda n: mult_x(n, None)),
+            TX0=("X", lambda n: turn_x(n, 0)),
+            TX1=("X", lambda n: turn_x(n, 1)),
+            EX0=("X", lambda n: empty_x(n, 0)),
+            EX1=("X", lambda n: empty_x(n, 1)),
             QX=("QX", quant_x),
-            mmA0=("QX", lambda n: mm_a(n, 0)),
-            mmA1=("QX", lambda n: mm_a(n, 1)),
-            sqA0=("QX", lambda n: square_a(n, 0)),
-            sqA1=("QX", lambda n: square_a(n, 1)),
+            mmA0=("MA", lambda n: mm_a(n, 0)),
+            mmA1=("MA", lambda n: mm_a(n, 1)),
+            sqA0=("MA", lambda n: square_a(n, 0)),
+            sqA1=("MA", lambda n: square_a(n, 1)),
             N0=("rec", lambda n: norm_a(n, 0)),
             N1=("rec", lambda n: norm_a(n, 1)),
             TC0=("rec", lambda n: turn_c(n, 0)),
             TC1=("rec", lambda n: turn_c(n, 1)),
             EC=("rec", empty_c),
             QC=("QC", quant_c),
-            mmQ0=("QC", lambda n: mm_q(n, 0)),
-            mmQ1=("QC", lambda n: mm_q(n, 1)),
-            R0=("R", lambda n: rope(n, 0)),
-            R1=("R", lambda n: rope(n, 1)),
-            add0=("R", lambda n: rope_add(n, 0, 1, ADD_ENG)),
-            add1=("R", lambda n: rope_add(n, 1, 2, ADD_ENG)),
-            add=("R", lambda n: rope_add(n, 0, 2, ADD_ENG)),
-            cpQ0=("cp", lambda n: copy_q(n, 0)),
-            cpQ1=("cp", lambda n: copy_q(n, 1)),
-            sqK=("cp", lambda n: (square_kv(n, 0), square_kv(n, 1))),
-            K=("ckv", lambda n: (ckv(n, 0), ckv(n, 1))),
+            mmR=("Q", mm_r),
+            mmN=("Q", mm_n),
+            R=("R", rope),
+            G=("R", gain_kv),
+            sqK=("R", square_kv),
+            add=("A", lambda n: rope_add(n, ADD_ENG)),
+            cpN=("cp", copy_n),
+            K=("ckv", ckv),
             store=("ckv", store),
         )
-        ADD_ENG = nc.vector
-        for s in range(PAIRS + LAG["ckv"]):
+        ADD_ENG, ND = nc.gpsimd, 4
+        INS = {(1, "G"): ("bq",), (1, "add"): ("t0",), (2, "add"): ("t1",)}
+        TAIL = "QX QC mmA0 R mmA1 sqA0 TX1 sqA1 sqrt TX0 EX1 M add EX0 mmR K G N0 mmN TC0 sqK N1 store TC1 cpN EC".split()
+        HEAD = "wS1 M b0 TX1 wV2 wS0 gq Mn TX0 EX0 dum EX1 wV3 wq0 b2 wq1 b3 b1".split()
+        def prepare(op):
+            if op == "M":
+                mult_x(0, None)
+            elif op == "Mn":
+                mult_x(1, None)
+            elif op in ("TX0", "TX1"):
+                turn_x(0, int(op[2]))
+            elif op in ("EX0", "EX1"):
+                empty_x(0, int(op[2]))
+            elif op in ("wS0", "wS1", "wS2", "wS3"):
+                wa_copy(nc.scalar.copy, int(op[2]) // 2, int(op[2]) % 2)
+            elif op in ("wV0", "wV1", "wV2", "wV3"):
+                wa_copy(nc.vector.tensor_copy, int(op[2]) // 2, int(op[2]) % 2)
+            elif op in ("wq0", "wq1"):
+                wa_quant(int(op[2]))
+            elif op == "gq":
+                prep_gq()
+            elif op == "dum":
+                dummies(ND)
+            elif op in ("b0", "b1", "b2", "b3"):
+                wb_copy(nc.scalar.copy, int(op[1]))
+            elif op == "bq":
+                wb_quants()
+            elif op in ("t0", "t1"):
+                tables(int(op[1]))
+        for op in HEAD:
+            prepare(op)
+        for s in range(1, PAIRS + LAG["ckv"]):
             has_a, has_k = 0 <= s - LAG["rec"] < PAIRS, 0 <= s - LAG["ckv"] < PAIRS
             lo, hi = (0 if has_a else 2), (4 if has_k else 2)
-            for op in ORDER:
-                if op in ("sqrt", "rec"):
+            for op in ORDER if s + 1 < PAIRS else TAIL:
+                if op == "sqrt":
                     if has_a or has_k:
-                        (sqrt if op == "sqrt" else recip)(s, lo, hi)
+                        sqrt(s, lo, hi)
+                    continue
+                if op == "tok":
+                    token(s + 1)
                     continue
                 lag = LAG[OPS[op][0]]
                 fn = OPS[op][1]
-                if op == "QC" and s == LAG["QC"]:
-                    wb_quants()
-                if 0 <= s - lag < PAIRS:
+                if op == "M":
+                    if s + 1 < PAIRS:
+                        fn(s + 1)
+                elif 0 <= s - lag < PAIRS:
                     fn(s - lag)
-                if s == 0 and op == "M1":
-                    first()
-                if s == 1 and op == "M0":
-                    wb_copies(nc.scalar.copy)
-                if s == 1 and op == "M1":
-                    negate_sin()
+                for extra in INS.get((s, op), ()):
+                    prepare(extra)

@@ -5,8 +5,9 @@ from concourse.masks import make_identity
 
 T, H, QR = 4096, 1024, 512
 NH, DN, DR, KVR = 2, 128, 64, 64
+HALF = DR // 2
 EPS = 1e-6
-OUT_W = 512
+OUT_W = NH * (DN + DR) + KVR + DR
 
 FLOPS = 2 * T * (H * (QR + KVR + DR) + QR * NH * (DN + DR))
 
@@ -23,6 +24,35 @@ FP8X4 = mybir.dt.float8_e4m3fn_x4
 MULT = mybir.AluOpType.mult
 ADD = mybir.AluOpType.add
 ACT = mybir.ActivationFunctionType
+
+STEP = """
+    rope a0 a1 quant_x square_kv square0 mult square1 turn1 add quant_c turn0 kv_rope rms empty1 gain
+    norm0 nope gate ckv norm1 empty0 turn_c0 copy store turn_c1 empty_c
+"""
+FIRST = """
+    mult:0 wa_scalar:1 turn0:0 wa_scalar:0 turn1:0 mult:1 wa_vector:2 wa_vector:3 gamma:0 empty0:0
+    turn0:1 empty1:0 quant_x:0 turn1:1 wb_copy:0 wa_quant:0 wb_copy:2 wb_copy:3 wa_quant:1 a0:0 empty1:1
+    square0:0 a1:0 mult:2 mult:3 square1:0 rms_a:0 norm0:0 dummies:4 turn1:2 empty0:1 wb_copy:1 turn0:2
+    turn_c0:0 empty1:2 table:1 empty0:2 norm1:0 quant_x:1 mult:4 turn_c1:0 wb_quant:0 a0:1 a1:1
+    empty_c:0 square0:1 turn1:3 quant_c:0 kv_rope:0 square1:1 rms_a:1 quant_x:2 table:0 turn0:3 nope:0
+    square_kv:0 norm1:1 norm0:1 empty0:3 mult:5 empty1:3 a1:2 turn_c0:1 square1:2 turn_c1:1 quant_x:3
+    gate:5 rope:0 a0:2 empty_c:1 turn0:4 square0:2 rms_a:2 turn1:4 quant_c:1 copy:0 gain:0 empty1:4
+    empty0:4 kv_rope:1 norm0:2 nope:1 norm1:2 turn_c0:2 copy:1 turn_c1:2 empty_c:2
+"""
+LAST = """
+    a0:-3 square0:-3 gain:-5 quant_x:-2 quant_c:-4 a1:-3 turn1:-1 nope:-4 turn0:-1 kv_rope:-4 square1:-3
+    rope:-5 rms_a:-3 norm0:-3 empty1:-1 norm1:-3 a0:-2 turn_c0:-3 copy:-4 empty0:-1 add:-6 turn_c1:-3
+    a1:-2 quant_x:-1 add:-5 a0:-1 square_kv:-5 rms_kv:-6 rope:-4 rms_kv:-5 square0:-2 empty_c:-3 gain:-4
+    square1:-2 quant_c:-3 a1:-1 rms_a:-2 kv_rope:-3 square0:-1 add:-4 nope:-3 norm0:-2 turn_c0:-2
+    norm1:-2 square1:-1 ckv:-5 gain:-3 rms_a:-1 square_kv:-3 store:-5 norm0:-1 turn_c1:-2 empty_c:-2
+    norm1:-1 turn_c0:-1 quant_c:-2 rope:-3 add_vector:-3 rms_kv:-3 square_kv:-4 copy:-3 turn_c1:-1
+    rms_kv:-4 kv_rope:-2 ckv:-6 store:-6 empty_c:-1 ckv:-4 quant_c:-1 nope:-2 kv_rope:-1 rope:-2 gain:-2
+    ckv:-3 add_vector:-2 nope:-1 copy:-2 square_kv:-2 rms_kv:-2 ckv:-2 rope:-1 store:-4 store:-3 copy:-1
+    gain:-1 store:-2 add_vector:-1 square_kv:-1 rms_kv:-1 ckv:-1 store:-1
+"""
+FIRST_STEP = 5
+NORM_LAG = 2
+KV_LAG = 5
 
 
 def tile_mla_model_t_kernel(
@@ -43,8 +73,8 @@ def tile_mla_model_t_kernel(
         ps_q = ctx.enter_context(tc.psum_pool(name="ps_q", bufs=1))
         ctx.enter_context(tc.manual_schedule())
 
-        xb = keep.tile([P, N_TILES * H], U8, name="xb")
-        scale8 = keep.tile([P, 2, 4], F32, name="scale8")
+        x_raw = keep.tile([P, N_TILES * H], U8, name="x_raw")
+        scale_raw = keep.tile([P, 2, 4], F32, name="scale_raw")
         scale = keep.tile([P, 2, H], F32, name="scale")
         wa_raw = keep.tile([P, 2, 4, QR], BF16, name="wa_raw")
         wkv_raw = keep.tile([P, 2, 4, KVR + DR], BF16, name="wkv_raw")
@@ -54,7 +84,7 @@ def tile_mla_model_t_kernel(
         gkv = keep.tile([P, KVR], BF16, name="gkv")
         cos = keep.tile([P, N_TILES, DR], BF16, name="cos")
         sin = keep.tile([P, N_TILES, DR], BF16, name="sin")
-        tab = keep.tile([P, N_TILES, 2, 2, DR // 2], BF16, name="tab")
+        factors = keep.tile([P, N_TILES, 2, 2, HALF], BF16, name="factors")
         ident = keep.tile([P, P], F32, name="ident")
         eps = keep.tile([P, 1], F32, name="eps")
         zero = keep.tile([P, 512], BF16, name="zero")
@@ -72,20 +102,16 @@ def tile_mla_model_t_kernel(
 
         def load_x(i0, i1):
             nc.sync.dma_start(
-                out=xb[:, i0 * H : i1 * H],
-                in_=x_hbm[:, i0:i1, :].rearrange("p i k -> p (i k)"),
+                out=x_raw[:, i0 * H : i1 * H], in_=x_hbm[:, i0:i1, :].rearrange("p i k -> p (i k)")
             )
 
         wa_hbm = wq_a.rearrange("(g p j) c -> g p j c", p=P, j=4)
-        nc.sync.dma_start(out=scale8[:], in_=x_scale.rearrange("o (h n c) -> n (o h) c", h=2, c=4))
-        for piece in "x0 x2 w0 w1".split():
-            if piece == "x0":
-                load_x(0, 2)
-            elif piece == "x2":
-                load_x(2, 4)
-            else:
-                nc.sync.dma_start(out=wa_raw[:, int(piece[1])], in_=wa_hbm[int(piece[1])])
         wkv_hbm = wkv.rearrange("(g p j) c -> g p j c", p=P, j=4)
+        nc.sync.dma_start(out=scale_raw[:], in_=x_scale.rearrange("o (h n c) -> n (o h) c", h=2, c=4))
+        load_x(0, 2)
+        load_x(2, 4)
+        nc.sync.dma_start(out=wa_raw[:, 0], in_=wa_hbm[0])
+        nc.sync.dma_start(out=wa_raw[:, 1], in_=wa_hbm[1])
         nc.sync.dma_start(out=wb_raw[:], in_=wq_b.rearrange("(p j) c -> p j c", j=4))
         nc.sync.dma_start(out=wkv_raw[:, 0], in_=wkv_hbm[0])
         nc.sync.dma_start(out=wkv_raw[:, 1], in_=wkv_hbm[1])
@@ -103,52 +129,63 @@ def tile_mla_model_t_kernel(
         nc.vector.memset(warm[:], 1.0)
         nc.scalar.activation(warm[:], warm[:], ACT.Abs_reciprocal_sqrt)
 
-        def dummies(k):
+        def dummies(count):
             bank = ps_q.tile([P, OUT_W], F32, name="pr", bufs=2)
-            for c in range(k):
+            for i in range(count):
                 nc.tensor.matmul(bank[:], lhsT=zero[:, 0:P], rhs=zero[:], start=True, stop=True)
 
         dummies(4)
-        for half in range(2):
+        for h in range(2):
             bank = ps_x.tile([P, 4, P], F32, name="xt")
             for c in range(4):
-                nc.tensor.transpose(
-                    bank[:, c, :], scale8[:, half, c : c + 1].to_broadcast([P, P]), ident[:]
-                )
+                nc.tensor.transpose(bank[:, c, :], scale_raw[:, h, c : c + 1].to_broadcast([P, P]), ident[:])
             for copy, j in ((nc.vector.tensor_copy, 0), (nc.scalar.copy, 1)):
                 copy(
-                    out=scale[:, j, 512 * half : 512 * (half + 1)].rearrange("p (n c) -> p n c", c=4),
+                    out=scale[:, j, 512 * h : 512 * (h + 1)].rearrange("p (n c) -> p n c", c=4),
                     in_=bank[:].rearrange("p c n -> p n c"),
                 )
 
         state = {}
 
-        def wa_copy(engine, g, u):
-            dst = wa_g[:].rearrange("p (g u m e j) -> p g u m e j", g=2, u=2, e=2, j=4)[:, g, u]
-            src = wa_raw[:, g].rearrange("p j (m u e) -> p u m e j", u=2, e=2)[:, u]
-            engine(out=dst, in_=src)
+
+        def wa_copy(engine, part):
+            g, u = divmod(part, 2)
+            engine(
+                out=wa_g[:].rearrange("p (g u m e j) -> p g u m e j", g=2, u=2, e=2, j=4)[:, g, u],
+                in_=wa_raw[:, g].rearrange("p j (m u e) -> p u m e j", u=2, e=2)[:, u],
+            )
 
         def wa_quant(g):
             nc.vector.quantize_mx(
                 out=wa_c[:, g, :].bitcast(FP8X4), scales=wa_s[:, g, :], in_=wa_g[:, g * 2048 : (g + 1) * 2048]
             )
 
-        def wb_copy(engine, part):
+        def gamma_copy(part):
+            nc.scalar.copy(
+                out=gq[:].rearrange("p (u m e) -> p u m e", u=2, e=2),
+                in_=gq_raw[:].rearrange("p (m u e) -> p u m e", u=2, e=2),
+            )
+
+        def wb_copy(part):
             wb_dst = wb_g[:].rearrange("p (c j) -> p c j", j=4)
-            wb_src = wb_raw[:].rearrange("p j (h c) -> p h c j", h=2)
+            wb_src = wb_raw[:].rearrange("p j (h c) -> p h c j", h=NH)
             kv_dst = wkv_g[:].rearrange("p (v g c j) -> p v g c j", v=2, g=2, j=4)
             kv_src = wkv_raw[:].rearrange("p g j c -> p g c j")
             if part == 0:
-                engine(out=wb_dst[:, 0:256].rearrange("p (h c) j -> p h c j", h=2), in_=wb_src[:, :, 0:DN])
+                nc.scalar.copy(
+                    out=wb_dst[:, 0:256].rearrange("p (h c) j -> p h c j", h=NH), in_=wb_src[:, :, 0:DN]
+                )
             elif part == 1:
-                engine(out=wb_dst[:, 256:384].rearrange("p (h c) j -> p h c j", h=2), in_=wb_src[:, :, DN:])
+                nc.scalar.copy(
+                    out=wb_dst[:, 256:384].rearrange("p (h c) j -> p h c j", h=NH), in_=wb_src[:, :, DN:]
+                )
             elif part == 2:
-                engine(out=kv_dst[:, 0], in_=kv_src)
+                nc.scalar.copy(out=kv_dst[:, 0], in_=kv_src)
             else:
-                engine(out=kv_dst[:, 1, :, 0:64], in_=kv_src[:, :, 64:128])
-                engine(out=kv_dst[:, 1, :, 64:128], in_=kv_src[:, :, 0:64])
+                nc.scalar.copy(out=kv_dst[:, 1, :, 0:64], in_=kv_src[:, :, 64:128])
+                nc.scalar.copy(out=kv_dst[:, 1, :, 64:128], in_=kv_src[:, :, 0:64])
 
-        def wb_quants():
+        def wb_quant(part):
             nc.vector.quantize_mx(
                 out=wkv_c[:].rearrange("p v g c -> p (v g c)").bitcast(FP8X4),
                 scales=wkv_s[:].rearrange("p v g c -> p (v g c)"),
@@ -157,25 +194,39 @@ def tile_mla_model_t_kernel(
             nc.vector.quantize_mx(out=wb_c[:, 0:256].bitcast(FP8X4), scales=wb_s[:, 0:256], in_=wb_g[:, 0:1024])
             nc.vector.quantize_mx(out=wb_c[:, 256:384].bitcast(FP8X4), scales=wb_s[:, 256:384], in_=wb_g[:, 1024:1536])
 
-        def mult_x(n, j):
-            if ("xs", n) not in state:
-                state["xs", n] = work.tile([P, 2 * H], BF16, name="xs", bufs=5)
-            xs = state["xs", n]
-            pieces = [(0, 2 * H)] if j is None else [(j * H, (j + 1) * H)]
-            if n == 0 and j != 1:
-                pieces = [(0, 512), (512, H)] + ([(H, 2 * H)] if j is None else [])
-            for k0, k1 in pieces:
+        def rope_table(part):
+            if part == 0:
+                nc.scalar.copy(out=factors[:, :, 0, 1, :], in_=sin[:, :, HALF:])
+                nc.scalar.activation(factors[:, :, 1, 0, :], sin[:, :, 0:HALF], ACT.Copy, scale=-1.0)
+            else:
+                nc.scalar.copy(out=factors[:, :, 0, 0, :], in_=cos[:, :, 0:HALF])
+                nc.scalar.copy(out=factors[:, :, 1, 1, :], in_=cos[:, :, HALF:])
+
+
+        def mult_x(n):
+            xs = work.tile([P, 2 * H], BF16, name="xs", bufs=5)
+            state["xs", n] = xs
+            if n == 0:
+                pieces = ((0, 0, 512), (0, 512, H), (1, 0, H))
+                for j, k0, k1 in pieces:
+                    nc.vector.tensor_tensor(
+                        out=xs[:, j * H + k0 : j * H + k1],
+                        in0=x_raw[:, j * H + k0 : j * H + k1].bitcast(FP8),
+                        in1=scale[:, 0, k0:k1],
+                        op=MULT,
+                    )
+            else:
                 nc.vector.tensor_tensor(
-                    out=xs[:, k0:k1],
-                    in0=xb[:, 2 * n * H + k0 : 2 * n * H + k1].bitcast(FP8),
-                    in1=scale[:].rearrange("p j k -> p (j k)")[:, k0 % H if n == 0 else k0 : (k1 - 1) % H + 1 if n == 0 else k1],
+                    out=xs[:],
+                    in0=x_raw[:, 2 * n * H : 2 * (n + 1) * H].bitcast(FP8),
+                    in1=scale[:].rearrange("p j k -> p (j k)"),
                     op=MULT,
                 )
 
-        def x_grouped(n):
-            if ("xg", n) not in state:
-                state["xg", n] = work.tile([P, 2048], BF16, name="xg", bufs=4, align_bytes=64)
-            return state["xg", n]
+        def gate(n):
+            if n < PAIRS:
+                seen = work.tile([P, 1], BF16, name="seen")
+                nc.gpsimd.tensor_copy(out=seen[:], in_=state["xs", n][:, 0:1])
 
         def turn_x(n, j):
             xt = ps_x.tile([P, 4, P], F32, name="xt")
@@ -186,7 +237,9 @@ def tile_mla_model_t_kernel(
             state["xt", n, j] = xt
 
         def empty_x(n, j):
-            view = x_grouped(n)[:].bitcast(F32).rearrange("p (j g n u) -> p j g n u", j=2, g=2, u=2)
+            if ("xg", n) not in state:
+                state["xg", n] = work.tile([P, 2 * H], BF16, name="xg", bufs=4, align_bytes=64)
+            view = state["xg", n][:].bitcast(F32).rearrange("p (j g n u) -> p j g n u", j=2, g=2, u=2)
             nc.scalar.copy(out=view[:, j], in_=state["xt", n, j][:].rearrange("p (g u) n -> p g n u", g=2))
 
         def quant_x(n):
@@ -195,13 +248,19 @@ def tile_mla_model_t_kernel(
             nc.vector.quantize_mx(out=xc[:].bitcast(FP8X4), scales=xsc[:], in_=state["xg", n][:])
             state["xc", n] = (xc, xsc)
 
+
         def mm_a(n, j):
             xc, xsc = state["xc", n]
-            pa = ps_a.tile([P, QR], F32, name="pa")
+            if n == PAIRS - 1:
+                bank = ps_x.tile([P, 4, P], F32, name="xt")
+                pa = bank[:].rearrange("p a b -> p (a b)")
+            else:
+                bank = ps_a.tile([P, QR], F32, name="pa")
+                pa = bank[:]
             for g in range(2):
                 cols = slice((2 * j + g) * P, (2 * j + g + 1) * P)
                 nc.tensor.matmul_mx(
-                    out=pa[:],
+                    out=pa,
                     lhsT=xc[:, cols].bitcast(FP8X4),
                     lhsT_scale=xsc[:, cols],
                     rhs=wa_c[:, g, :].bitcast(FP8X4),
@@ -217,30 +276,33 @@ def tile_mla_model_t_kernel(
             return state[kind, s]
 
         def square_a(n, j):
-            junk = work.tile([P, QR], BF16, name="junk")
-            ss = stat("ss", n + LAG["rec"])
-            nc.scalar.activation(junk[:], state["pa", n, j][:], ACT.Square, scale=QR**-0.5, accum_out=ss[:, j : j + 1])
+            squares = work.tile([P, QR], BF16, name="squares_a")
+            mean = stat("mean", n + NORM_LAG)
+            nc.scalar.activation(
+                squares[:], state["pa", n, j], ACT.Square, scale=QR**-0.5, accum_out=mean[:, j : j + 1]
+            )
 
-        def sqrt(s, lo, hi):
-            nc.scalar.activation(stat("rinv", s)[:, lo:hi], stat("ss", s)[:, lo:hi], ACT.Abs_reciprocal_sqrt, bias=eps[:])
-
+        def inverse_rms(s, c0, c1):
+            nc.scalar.activation(
+                stat("rinv", s)[:, c0:c1], stat("mean", s)[:, c0:c1], ACT.Abs_reciprocal_sqrt, bias=eps[:]
+            )
 
         def norm_a(n, j):
-            cqs = work.tile([P, QR], BF16, name="cqs", bufs=4)
+            cq = work.tile([P, QR], BF16, name="cq", bufs=4)
             nc.vector.scalar_tensor_tensor(
-                out=cqs[:],
-                in0=state["pa", n, j][:],
-                scalar=stat("rinv", n + LAG["rec"])[:, j : j + 1],
+                out=cq[:],
+                in0=state["pa", n, j],
+                scalar=stat("rinv", n + NORM_LAG)[:, j : j + 1],
                 in1=gq[:],
                 op0=MULT,
                 op1=MULT,
             )
-            state["cqs", n, j] = cqs
+            state["cq", n, j] = cq
 
         def turn_c(n, j):
             if j == 0:
                 state["ct", n] = ps_c.tile([P, 2, 2, P], F32, name="ct")
-            words = state["cqs", n, j][:].bitcast(F32)
+            words = state["cq", n, j][:].bitcast(F32)
             for u in range(2):
                 nc.tensor.transpose(state["ct", n][:, j, u, :], words[:, u * P : (u + 1) * P], ident[:])
 
@@ -258,7 +320,8 @@ def tile_mla_model_t_kernel(
             nc.vector.quantize_mx(out=cc[:].bitcast(FP8X4), scales=cs[:], in_=state["cg", n][:])
             state["cc", n] = (cc, cs)
 
-        def mm_r(n):
+
+        def mm_kv_rope(n):
             cc, cs = state["cc", n]
             xc, xsc = state["xc", n]
             pr = ps_q.tile([P, OUT_W], F32, name="pr", bufs=2)
@@ -286,7 +349,7 @@ def tile_mla_model_t_kernel(
                 )
             state["pr", n] = pr
 
-        def mm_n(n):
+        def mm_nope(n):
             cc, cs = state["cc", n]
             pn = ps_q.tile([P, 2, 256], F32, name="pn", bufs=1)
             for j in range(2):
@@ -302,76 +365,73 @@ def tile_mla_model_t_kernel(
                 )
             state["pn", n] = pn
 
+
         def out_tile(n):
             if ("ot", n) not in state:
                 state["ot", n] = work.tile([P, 1152], F32, name="ot", bufs=6)
             return state["ot", n]
 
-        def copy_n(n):
+        def copy_nope(n):
             nc.scalar.copy(
-                out=out_tile(n)[:, 128:896].rearrange("p (h c) -> p h c", c=192)[:, :, 0:DN],
-                in_=state["pn", n][:].rearrange("p j (h c) -> p (j h) c", h=2),
+                out=out_tile(n)[:, 128:896].rearrange("p (h c) -> p h c", c=DN + DR)[:, :, 0:DN],
+                in_=state["pn", n][:].rearrange("p j (h c) -> p (j h) c", h=NH),
             )
 
-        def ckv_cols(tile, stride, n):
-            return tile[:, 0 : 2 * stride].rearrange("p (j c) -> p j c", j=2)[:, :, 0:n]
-
         def square_kv(n):
-            ss = stat("ss", n + LAG["ckv"])
+            mean = stat("mean", n + KV_LAG)
             for j in range(2):
-                junk = work.tile([P, KVR], BF16, name="junk2")
+                squares = work.tile([P, KVR], BF16, name="squares_kv")
                 nc.scalar.activation(
-                    junk[:], state["pr", n][:, 448 * j : 448 * j + 64], ACT.Square, scale=KVR**-0.5, accum_out=ss[:, 2 + j : 3 + j]
+                    squares[:],
+                    state["pr", n][:, 448 * j : 448 * j + KVR],
+                    ACT.Square,
+                    scale=KVR**-0.5,
+                    accum_out=mean[:, 2 + j : 3 + j],
                 )
 
         def gain_kv(n):
-            gv = work.tile([P, 2, KVR], F32, name="gv", bufs=5)
+            gained = work.tile([P, 2, KVR], F32, name="gained", bufs=5)
             nc.vector.tensor_tensor(
-                out=gv[:],
-                in0=state["pr", n][:].rearrange("p (b c) -> p b c", c=64)[:, 0:8:7, :],
+                out=gained[:],
+                in0=state["pr", n][:].rearrange("p (b c) -> p b c", c=KVR)[:, 0:8:7, :],
                 in1=gkv[:].unsqueeze(1).to_broadcast([P, 2, KVR]),
                 op=MULT,
             )
-            state["gv", n] = gv
+            state["gained", n] = gained
 
-        def rope(n):
-            mt = work.tile([P, 6, 2, 2, 32], F32, name="mt", bufs=4)
+        def scale_ckv(n):
+            for j in range(2):
+                nc.scalar.activation(
+                    out_tile(n)[:, 960 * j : 960 * j + KVR],
+                    state["gained", n][:, j, :],
+                    ACT.Copy,
+                    scale=stat("rinv", n + KV_LAG)[:, 2 + j : 3 + j],
+                )
+
+        def rope_products(n):
+            products = work.tile([P, 6, 2, 2, HALF], F32, name="products", bufs=4)
             nc.vector.tensor_tensor(
-                out=mt[:].rearrange("p (j s) h w d -> p j s h w d", j=2),
+                out=products[:].rearrange("p (j s) h w d -> p j s h w d", j=2),
                 in0=state["pr", n][:, 64:448]
                 .rearrange("p (j s h d) -> p j s h d", j=2, s=3, h=2)
                 .unsqueeze(4)
-                .to_broadcast([P, 2, 3, 2, 2, 32]),
-                in1=tab[:, 2 * n : 2 * n + 2].unsqueeze(2).to_broadcast([P, 2, 3, 2, 2, 32]),
+                .to_broadcast([P, 2, 3, 2, 2, HALF]),
+                in1=factors[:, 2 * n : 2 * n + 2].unsqueeze(2).to_broadcast([P, 2, 3, 2, 2, HALF]),
                 op=MULT,
             )
-            state["mt", n] = mt
-
-        def token(n):
-            if 0 < n < PAIRS:
-                tok = work.tile([P, 1], BF16, name="tok")
-                nc.gpsimd.tensor_copy(out=tok[:], in_=state["xs", n][:, 0:1])
+            state["products", n] = products
 
         def rope_add(n, engine):
-            mt = state["mt", n][:].rearrange("p s h w d -> p s h (w d)")
+            products = state["products", n][:].rearrange("p s h w d -> p s h (w d)")
             engine.tensor_tensor(
-                out=out_tile(n)[:].rearrange("p (s c) -> p s c", c=192)[:, :, 64:128],
-                in0=mt[:, :, 0, :],
-                in1=mt[:, :, 1, :],
+                out=out_tile(n)[:].rearrange("p (s c) -> p s c", c=DN + DR)[:, :, 64:128],
+                in0=products[:, :, 0, :],
+                in1=products[:, :, 1, :],
                 op=ADD,
             )
 
-        def ckv(n):
-            for j in range(2):
-                nc.scalar.activation(
-                    state["ot", n][:, 960 * j : 960 * j + 64],
-                    state["gv", n][:, j, :],
-                    ACT.Copy,
-                    scale=stat("rinv", n + LAG["ckv"])[:, 2 + j : 3 + j],
-                )
-
         def store(n):
-            ot = state["ot", n]
+            ot = out_tile(n)
             nc.sync.dma_start(
                 out=out_hbm[:, 2 * n : 2 * n + 2, 0:384], in_=ot[:, 128:896].rearrange("p (j c) -> p j c", j=2)
             )
@@ -380,97 +440,53 @@ def tile_mla_model_t_kernel(
                 in_=ot[:].rearrange("p (b c) -> p b c", c=192)[:, 0:6:5, 0:128],
             )
 
-        def prep_gq():
-            nc.scalar.copy(
-                out=gq[:].rearrange("p (u m e) -> p u m e", u=2, e=2),
-                in_=gq_raw[:].rearrange("p (m u e) -> p u m e", u=2, e=2),
-            )
-
-        def tables(half):
-            if half == 0:
-                nc.scalar.copy(out=tab[:, :, 0, 1, :], in_=sin[:, :, 32:64])
-                nc.scalar.activation(tab[:, :, 1, 0, :], sin[:, :, 0:32], ACT.Copy, scale=-1.0)
-            else:
-                nc.scalar.copy(out=tab[:, :, 0, 0, :], in_=cos[:, :, 0:32])
-                nc.scalar.copy(out=tab[:, :, 1, 1, :], in_=cos[:, :, 32:64])
-
-        LAG = {'M': 0, 'X': 0, 'QX': 1, 'MA': 1, 'rec': 1, 'QC': 2, 'Q': 2, 'R': 3, 'A': 3, 'cp': 2, 'ckv': 4}
-        ORDER = "QX mmA0 mmA1 TX0 TX1 sqA0 M sqA1 sqrt R QC EX0 EX1 G mmR sqK K N0 mmN cpN TC0 N1 store add TC1 EC".split()
         OPS = dict(
-            M=("M", lambda n: mult_x(n, None)),
-            TX0=("X", lambda n: turn_x(n, 0)),
-            TX1=("X", lambda n: turn_x(n, 1)),
-            EX0=("X", lambda n: empty_x(n, 0)),
-            EX1=("X", lambda n: empty_x(n, 1)),
-            QX=("QX", quant_x),
-            mmA0=("MA", lambda n: mm_a(n, 0)),
-            mmA1=("MA", lambda n: mm_a(n, 1)),
-            sqA0=("MA", lambda n: square_a(n, 0)),
-            sqA1=("MA", lambda n: square_a(n, 1)),
-            N0=("rec", lambda n: norm_a(n, 0)),
-            N1=("rec", lambda n: norm_a(n, 1)),
-            TC0=("rec", lambda n: turn_c(n, 0)),
-            TC1=("rec", lambda n: turn_c(n, 1)),
-            EC=("rec", empty_c),
-            QC=("QC", quant_c),
-            mmR=("Q", mm_r),
-            mmN=("Q", mm_n),
-            R=("R", rope),
-            G=("R", gain_kv),
-            sqK=("R", square_kv),
-            add=("A", lambda n: rope_add(n, ADD_ENG)),
-            cpN=("cp", copy_n),
-            K=("ckv", ckv),
-            store=("ckv", store),
+            mult=(-1, mult_x),
+            gate=(-1, gate),
+            turn0=(0, lambda n: turn_x(n, 0)),
+            turn1=(0, lambda n: turn_x(n, 1)),
+            empty0=(0, lambda n: empty_x(n, 0)),
+            empty1=(0, lambda n: empty_x(n, 1)),
+            quant_x=(1, quant_x),
+            a0=(NORM_LAG, lambda n: mm_a(n, 0)),
+            a1=(NORM_LAG, lambda n: mm_a(n, 1)),
+            square0=(NORM_LAG, lambda n: square_a(n, 0)),
+            square1=(NORM_LAG, lambda n: square_a(n, 1)),
+            norm0=(NORM_LAG, lambda n: norm_a(n, 0)),
+            norm1=(NORM_LAG, lambda n: norm_a(n, 1)),
+            turn_c0=(NORM_LAG, lambda n: turn_c(n, 0)),
+            turn_c1=(NORM_LAG, lambda n: turn_c(n, 1)),
+            empty_c=(NORM_LAG, empty_c),
+            quant_c=(3, quant_c),
+            kv_rope=(3, mm_kv_rope),
+            nope=(3, mm_nope),
+            copy=(3, copy_nope),
+            rope=(4, rope_products),
+            gain=(4, gain_kv),
+            square_kv=(4, square_kv),
+            add=(5, lambda n: rope_add(n, nc.gpsimd)),
+            add_vector=(5, lambda n: rope_add(n, nc.vector)),
+            ckv=(KV_LAG, scale_ckv),
+            store=(5, store),
+            rms=(0, lambda s: inverse_rms(s, 0, 4)),
+            rms_a=(0, lambda n: inverse_rms(n + NORM_LAG, 0, 2)),
+            rms_kv=(0, lambda n: inverse_rms(n + KV_LAG, 2, 4)),
+            wa_scalar=(0, lambda part: wa_copy(nc.scalar.copy, part)),
+            wa_vector=(0, lambda part: wa_copy(nc.vector.tensor_copy, part)),
+            wa_quant=(0, wa_quant),
+            gamma=(0, gamma_copy),
+            wb_copy=(0, wb_copy),
+            wb_quant=(0, wb_quant),
+            table=(0, rope_table),
+            dummies=(0, dummies),
         )
-        ADD_ENG, ND = nc.gpsimd, 4
-        INS = {(1, "G"): ("bq",), (1, "add"): ("t0",), (2, "add"): ("t1",)}
-        TAIL = "QX QC mmA0 R mmA1 sqA0 TX1 sqA1 sqrt TX0 EX1 M add EX0 mmR K G N0 mmN TC0 sqK N1 store TC1 cpN EC".split()
-        HEAD = "wS1 M b0 TX1 wV2 wS0 gq Mn TX0 EX0 dum EX1 wV3 wq0 b2 wq1 b3 b1".split()
-        def prepare(op):
-            if op == "M":
-                mult_x(0, None)
-            elif op == "Mn":
-                mult_x(1, None)
-            elif op in ("TX0", "TX1"):
-                turn_x(0, int(op[2]))
-            elif op in ("EX0", "EX1"):
-                empty_x(0, int(op[2]))
-            elif op in ("wS0", "wS1", "wS2", "wS3"):
-                wa_copy(nc.scalar.copy, int(op[2]) // 2, int(op[2]) % 2)
-            elif op in ("wV0", "wV1", "wV2", "wV3"):
-                wa_copy(nc.vector.tensor_copy, int(op[2]) // 2, int(op[2]) % 2)
-            elif op in ("wq0", "wq1"):
-                wa_quant(int(op[2]))
-            elif op == "gq":
-                prep_gq()
-            elif op == "dum":
-                dummies(ND)
-            elif op in ("b0", "b1", "b2", "b3"):
-                wb_copy(nc.scalar.copy, int(op[1]))
-            elif op == "bq":
-                wb_quants()
-            elif op in ("t0", "t1"):
-                tables(int(op[1]))
-        for op in HEAD:
-            prepare(op)
-        for s in range(1, PAIRS + LAG["ckv"]):
-            has_a, has_k = 0 <= s - LAG["rec"] < PAIRS, 0 <= s - LAG["ckv"] < PAIRS
-            lo, hi = (0 if has_a else 2), (4 if has_k else 2)
-            for op in ORDER if s + 1 < PAIRS else TAIL:
-                if op == "sqrt":
-                    if has_a or has_k:
-                        sqrt(s, lo, hi)
-                    continue
-                if op == "tok":
-                    token(s + 1)
-                    continue
-                lag = LAG[OPS[op][0]]
-                fn = OPS[op][1]
-                if op == "M":
-                    if s + 1 < PAIRS:
-                        fn(s + 1)
-                elif 0 <= s - lag < PAIRS:
-                    fn(s - lag)
-                for extra in INS.get((s, op), ()):
-                    prepare(extra)
+        for word in FIRST.split():
+            stage, number = word.split(":")
+            OPS[stage][1](int(number))
+        for s in range(FIRST_STEP, PAIRS - 1):
+            for stage in STEP.split():
+                lag, run = OPS[stage]
+                run(s - lag)
+        for word in LAST.split():
+            stage, number = word.split(":")
+            OPS[stage][1](PAIRS + int(number))

from contextlib import ExitStack

import concourse.mybir as mybir
from concourse.masks import make_identity

T, H, QR = 4096, 1024, 512
NH, DN, DR, KVR = 2, 128, 64, 64
HALF = DR // 2
EPS = 1e-6
OUT_W = NH * (DN + DR) + KVR + DR

FLOPS = 2 * T * (H * (QR + KVR + DR) + QR * NH * (DN + DR))

P = 128
N_TILES = T // P
PAIRS = N_TILES // 2

F32 = mybir.dt.float32
BF16 = mybir.dt.bfloat16
U32 = mybir.dt.uint32
U8 = mybir.dt.uint8
FP8 = mybir.dt.float8_e4m3fn
FP8X4 = mybir.dt.float8_e4m3fn_x4
MULT = mybir.AluOpType.mult
ADD = mybir.AluOpType.add
ACT = mybir.ActivationFunctionType

STEP = """
    rope a0 a1 quant_x square_kv square0 mult square1 turn1 add quant_c turn0 kv_rope rms empty1 gain
    norm0 nope gate ckv norm1 empty0 turn_c0 copy store turn_c1 empty_c
"""
FIRST = """
    mult:0 wa_scalar:1 turn0:0 wa_scalar:0 turn1:0 mult:1 wa_vector:2 wa_vector:3 gamma:0 empty0:0
    turn0:1 empty1:0 quant_x:0 turn1:1 wb_copy:0 wa_quant:0 wb_copy:2 wb_copy:3 wa_quant:1 a0:0 empty1:1
    square0:0 a1:0 mult:2 mult:3 square1:0 rms_a:0 norm0:0 dummies:4 turn1:2 empty0:1 wb_copy:1 turn0:2
    turn_c0:0 empty1:2 table:1 empty0:2 norm1:0 quant_x:1 mult:4 turn_c1:0 wb_quant:0 a0:1 a1:1
    empty_c:0 square0:1 turn1:3 quant_c:0 kv_rope:0 square1:1 rms_a:1 quant_x:2 table:0 turn0:3 nope:0
    square_kv:0 norm1:1 norm0:1 empty0:3 mult:5 empty1:3 a1:2 turn_c0:1 square1:2 turn_c1:1 quant_x:3
    gate:5 rope:0 a0:2 empty_c:1 turn0:4 square0:2 rms_a:2 turn1:4 quant_c:1 copy:0 gain:0 empty1:4
    empty0:4 kv_rope:1 norm0:2 nope:1 norm1:2 turn_c0:2 copy:1 turn_c1:2 empty_c:2
"""
LAST = """
    a0:-3 square0:-3 gain:-5 quant_x:-2 quant_c:-4 a1:-3 turn1:-1 nope:-4 turn0:-1 kv_rope:-4 square1:-3
    rope:-5 rms_a:-3 norm0:-3 empty1:-1 norm1:-3 a0:-2 turn_c0:-3 copy:-4 empty0:-1 add:-6 turn_c1:-3
    a1:-2 quant_x:-1 add:-5 a0:-1 square_kv:-5 rms_kv:-6 rope:-4 rms_kv:-5 square0:-2 empty_c:-3 gain:-4
    square1:-2 quant_c:-3 a1:-1 rms_a:-2 kv_rope:-3 square0:-1 add:-4 nope:-3 norm0:-2 turn_c0:-2
    norm1:-2 square1:-1 ckv:-5 gain:-3 rms_a:-1 square_kv:-3 store:-5 norm0:-1 turn_c1:-2 empty_c:-2
    norm1:-1 turn_c0:-1 quant_c:-2 rope:-3 add_vector:-3 rms_kv:-3 square_kv:-4 copy:-3 turn_c1:-1
    rms_kv:-4 kv_rope:-2 ckv:-6 store:-6 empty_c:-1 ckv:-4 quant_c:-1 nope:-2 kv_rope:-1 rope:-2 gain:-2
    ckv:-3 add_vector:-2 nope:-1 copy:-2 square_kv:-2 rms_kv:-2 ckv:-2 rope:-1 store:-4 store:-3 copy:-1
    gain:-1 store:-2 add_vector:-1 square_kv:-1 rms_kv:-1 ckv:-1 store:-1
"""
FIRST_STEP = 5
NORM_LAG = 2
KV_LAG = 5


def tile_mla_model_t_kernel(
    tc, x_bytes, x_scale, wq_a, wq_b, wkv, rope_cos, rope_sin, gamma_cq, gamma_ckv, out
):
    nc = tc.nc
    x_hbm = x_bytes.rearrange("(p i) k -> p i k", i=N_TILES)
    cos_hbm = rope_cos.rearrange("(p i) d -> p i d", i=N_TILES)
    sin_hbm = rope_sin.rearrange("(p i) d -> p i d", i=N_TILES)
    out_hbm = out.rearrange("(p i) c -> p i c", i=N_TILES)

    with ExitStack() as ctx:
        keep = ctx.enter_context(tc.tile_pool(name="keep", bufs=1))
        work = ctx.enter_context(tc.tile_pool(name="work", bufs=2))
        ps_x = ctx.enter_context(tc.psum_pool(name="ps_x", bufs=2))
        ps_a = ctx.enter_context(tc.psum_pool(name="ps_a", bufs=2))
        ps_c = ctx.enter_context(tc.psum_pool(name="ps_c", bufs=1))
        ps_q = ctx.enter_context(tc.psum_pool(name="ps_q", bufs=1))
        ctx.enter_context(tc.manual_schedule())

        x_raw = keep.tile([P, N_TILES * H], U8, name="x_raw")
        scale_raw = keep.tile([P, 2, 4], F32, name="scale_raw")
        scale = keep.tile([P, 2, H], F32, name="scale")
        wa_raw = keep.tile([P, 2, 4, QR], BF16, name="wa_raw")
        wkv_raw = keep.tile([P, 2, 4, KVR + DR], BF16, name="wkv_raw")
        wb_raw = keep.tile([P, 4, NH * (DN + DR)], BF16, name="wb_raw")
        gq_raw = keep.tile([P, QR], BF16, name="gq_raw")
        gq = keep.tile([P, QR], BF16, name="gq")
        gkv = keep.tile([P, KVR], BF16, name="gkv")
        cos = keep.tile([P, N_TILES, DR], BF16, name="cos")
        sin = keep.tile([P, N_TILES, DR], BF16, name="sin")
        factors = keep.tile([P, N_TILES, 2, 2, HALF], BF16, name="factors")
        ident = keep.tile([P, P], F32, name="ident")
        eps = keep.tile([P, 1], F32, name="eps")
        zero = keep.tile([P, 512], BF16, name="zero")
        warm = keep.tile([P, 1], F32, name="warm")

        wa_g = keep.tile([P, 2 * QR * 4], BF16, name="wa_g", align_bytes=64)
        wa_c = keep.tile([P, 2, QR], U32, name="wa_c", align_bytes=64)
        wa_s = keep.tile([P, 2, QR], U8, name="wa_s", align_bytes=64)
        wkv_g = keep.tile([P, 4 * 128 * 4], BF16, name="wkv_g", align_bytes=64)
        wkv_c = keep.tile([P, 2, 2, 128], U32, name="wkv_c", align_bytes=64)
        wkv_s = keep.tile([P, 2, 2, 128], U8, name="wkv_s", align_bytes=64)
        wb_g = keep.tile([P, 384 * 4], BF16, name="wb_g", align_bytes=64)
        wb_c = keep.tile([P, 384], U32, name="wb_c", align_bytes=64)
        wb_s = keep.tile([P, 384], U8, name="wb_s", align_bytes=64)

        def load_x(i0, i1):
            nc.sync.dma_start(
                out=x_raw[:, i0 * H : i1 * H], in_=x_hbm[:, i0:i1, :].rearrange("p i k -> p (i k)")
            )

        wa_hbm = wq_a.rearrange("(g p j) c -> g p j c", p=P, j=4)
        wkv_hbm = wkv.rearrange("(g p j) c -> g p j c", p=P, j=4)
        nc.sync.dma_start(out=scale_raw[:], in_=x_scale.rearrange("o (h n c) -> n (o h) c", h=2, c=4))
        load_x(0, 2)
        load_x(2, 4)
        nc.sync.dma_start(out=wa_raw[:, 0], in_=wa_hbm[0])
        nc.sync.dma_start(out=wa_raw[:, 1], in_=wa_hbm[1])
        nc.sync.dma_start(out=wb_raw[:], in_=wq_b.rearrange("(p j) c -> p j c", j=4))
        nc.sync.dma_start(out=wkv_raw[:, 0], in_=wkv_hbm[0])
        nc.sync.dma_start(out=wkv_raw[:, 1], in_=wkv_hbm[1])
        nc.sync.dma_start(out=gq_raw[:], in_=gamma_cq.partition_broadcast(P))
        nc.sync.dma_start(out=sin[:], in_=sin_hbm)
        nc.sync.dma_start(out=cos[:], in_=cos_hbm)
        load_x(4, 8)
        nc.sync.dma_start(out=gkv[:], in_=gamma_ckv.partition_broadcast(P))
        for i0 in range(8, N_TILES, 4):
            load_x(i0, i0 + 4)

        make_identity(nc, ident[:])
        nc.gpsimd.memset(zero[:], 0.0)
        nc.vector.memset(eps[:], EPS)
        nc.vector.memset(warm[:], 1.0)
        nc.scalar.activation(warm[:], warm[:], ACT.Abs_reciprocal_sqrt)

        def dummies(count):
            bank = ps_q.tile([P, OUT_W], F32, name="pr", bufs=2)
            for i in range(count):
                nc.tensor.matmul(bank[:], lhsT=zero[:, 0:P], rhs=zero[:], start=True, stop=True)

        dummies(4)
        for h in range(2):
            bank = ps_x.tile([P, 4, P], F32, name="xt")
            for c in range(4):
                nc.tensor.transpose(bank[:, c, :], scale_raw[:, h, c : c + 1].to_broadcast([P, P]), ident[:])
            for copy, j in ((nc.vector.tensor_copy, 0), (nc.scalar.copy, 1)):
                copy(
                    out=scale[:, j, 512 * h : 512 * (h + 1)].rearrange("p (n c) -> p n c", c=4),
                    in_=bank[:].rearrange("p c n -> p n c"),
                )

        state = {}


        def wa_copy(engine, part):
            g, u = divmod(part, 2)
            engine(
                out=wa_g[:].rearrange("p (g u m e j) -> p g u m e j", g=2, u=2, e=2, j=4)[:, g, u],
                in_=wa_raw[:, g].rearrange("p j (m u e) -> p u m e j", u=2, e=2)[:, u],
            )

        def wa_quant(g):
            nc.vector.quantize_mx(
                out=wa_c[:, g, :].bitcast(FP8X4), scales=wa_s[:, g, :], in_=wa_g[:, g * 2048 : (g + 1) * 2048]
            )

        def gamma_copy(part):
            nc.scalar.copy(
                out=gq[:].rearrange("p (u m e) -> p u m e", u=2, e=2),
                in_=gq_raw[:].rearrange("p (m u e) -> p u m e", u=2, e=2),
            )

        def wb_copy(part):
            wb_dst = wb_g[:].rearrange("p (c j) -> p c j", j=4)
            wb_src = wb_raw[:].rearrange("p j (h c) -> p h c j", h=NH)
            kv_dst = wkv_g[:].rearrange("p (v g c j) -> p v g c j", v=2, g=2, j=4)
            kv_src = wkv_raw[:].rearrange("p g j c -> p g c j")
            if part == 0:
                nc.scalar.copy(
                    out=wb_dst[:, 0:256].rearrange("p (h c) j -> p h c j", h=NH), in_=wb_src[:, :, 0:DN]
                )
            elif part == 1:
                nc.scalar.copy(
                    out=wb_dst[:, 256:384].rearrange("p (h c) j -> p h c j", h=NH), in_=wb_src[:, :, DN:]
                )
            elif part == 2:
                nc.scalar.copy(out=kv_dst[:, 0], in_=kv_src)
            else:
                nc.scalar.copy(out=kv_dst[:, 1, :, 0:64], in_=kv_src[:, :, 64:128])
                nc.scalar.copy(out=kv_dst[:, 1, :, 64:128], in_=kv_src[:, :, 0:64])

        def wb_quant(part):
            nc.vector.quantize_mx(
                out=wkv_c[:].rearrange("p v g c -> p (v g c)").bitcast(FP8X4),
                scales=wkv_s[:].rearrange("p v g c -> p (v g c)"),
                in_=wkv_g[:],
            )
            nc.vector.quantize_mx(out=wb_c[:, 0:256].bitcast(FP8X4), scales=wb_s[:, 0:256], in_=wb_g[:, 0:1024])
            nc.vector.quantize_mx(out=wb_c[:, 256:384].bitcast(FP8X4), scales=wb_s[:, 256:384], in_=wb_g[:, 1024:1536])

        def rope_table(part):
            if part == 0:
                nc.scalar.copy(out=factors[:, :, 0, 1, :], in_=sin[:, :, HALF:])
                nc.scalar.activation(factors[:, :, 1, 0, :], sin[:, :, 0:HALF], ACT.Copy, scale=-1.0)
            else:
                nc.scalar.copy(out=factors[:, :, 0, 0, :], in_=cos[:, :, 0:HALF])
                nc.scalar.copy(out=factors[:, :, 1, 1, :], in_=cos[:, :, HALF:])


        def mult_x(n):
            xs = work.tile([P, 2 * H], BF16, name="xs", bufs=5)
            state["xs", n] = xs
            if n == 0:
                pieces = ((0, 0, 512), (0, 512, H), (1, 0, H))
                for j, k0, k1 in pieces:
                    nc.vector.tensor_tensor(
                        out=xs[:, j * H + k0 : j * H + k1],
                        in0=x_raw[:, j * H + k0 : j * H + k1].bitcast(FP8),
                        in1=scale[:, 0, k0:k1],
                        op=MULT,
                    )
            else:
                nc.vector.tensor_tensor(
                    out=xs[:],
                    in0=x_raw[:, 2 * n * H : 2 * (n + 1) * H].bitcast(FP8),
                    in1=scale[:].rearrange("p j k -> p (j k)"),
                    op=MULT,
                )

        def gate(n):
            if n < PAIRS:
                seen = work.tile([P, 1], BF16, name="seen")
                nc.gpsimd.tensor_copy(out=seen[:], in_=state["xs", n][:, 0:1])

        def turn_x(n, j):
            xt = ps_x.tile([P, 4, P], F32, name="xt")
            words = state["xs", n][:, j * H : (j + 1) * H].bitcast(F32)
            for g in range(2):
                for u in range(2):
                    nc.tensor.transpose(xt[:, 2 * g + u, :], words[:, 256 * g + u : 256 * (g + 1) : 2], ident[:])
            state["xt", n, j] = xt

        def empty_x(n, j):
            if ("xg", n) not in state:
                state["xg", n] = work.tile([P, 2 * H], BF16, name="xg", bufs=4, align_bytes=64)
            view = state["xg", n][:].bitcast(F32).rearrange("p (j g n u) -> p j g n u", j=2, g=2, u=2)
            nc.scalar.copy(out=view[:, j], in_=state["xt", n, j][:].rearrange("p (g u) n -> p g n u", g=2))

        def quant_x(n):
            xc = work.tile([P, 512], U32, name="xc", bufs=7, align_bytes=64)
            xsc = work.tile([P, 512], U8, name="xsc", bufs=7, align_bytes=64)
            nc.vector.quantize_mx(out=xc[:].bitcast(FP8X4), scales=xsc[:], in_=state["xg", n][:])
            state["xc", n] = (xc, xsc)


        def mm_a(n, j):
            xc, xsc = state["xc", n]
            if n == PAIRS - 1:
                bank = ps_x.tile([P, 4, P], F32, name="xt")
                pa = bank[:].rearrange("p a b -> p (a b)")
            else:
                bank = ps_a.tile([P, QR], F32, name="pa")
                pa = bank[:]
            for g in range(2):
                cols = slice((2 * j + g) * P, (2 * j + g + 1) * P)
                nc.tensor.matmul_mx(
                    out=pa,
                    lhsT=xc[:, cols].bitcast(FP8X4),
                    lhsT_scale=xsc[:, cols],
                    rhs=wa_c[:, g, :].bitcast(FP8X4),
                    rhs_scale=wa_s[:, g, :],
                    start=(g == 0),
                    stop=(g == 1),
                )
            state["pa", n, j] = pa

        def stat(kind, s):
            if (kind, s) not in state:
                state[kind, s] = work.tile([P, 4], F32, name=kind, bufs=6)
            return state[kind, s]

        def square_a(n, j):
            squares = work.tile([P, QR], BF16, name="squares_a")
            mean = stat("mean", n + NORM_LAG)
            nc.scalar.activation(
                squares[:], state["pa", n, j], ACT.Square, scale=QR**-0.5, accum_out=mean[:, j : j + 1]
            )

        def inverse_rms(s, c0, c1):
            nc.scalar.activation(
                stat("rinv", s)[:, c0:c1], stat("mean", s)[:, c0:c1], ACT.Abs_reciprocal_sqrt, bias=eps[:]
            )

        def norm_a(n, j):
            cq = work.tile([P, QR], BF16, name="cq", bufs=4)
            nc.vector.scalar_tensor_tensor(
                out=cq[:],
                in0=state["pa", n, j],
                scalar=stat("rinv", n + NORM_LAG)[:, j : j + 1],
                in1=gq[:],
                op0=MULT,
                op1=MULT,
            )
            state["cq", n, j] = cq

        def turn_c(n, j):
            if j == 0:
                state["ct", n] = ps_c.tile([P, 2, 2, P], F32, name="ct")
            words = state["cq", n, j][:].bitcast(F32)
            for u in range(2):
                nc.tensor.transpose(state["ct", n][:, j, u, :], words[:, u * P : (u + 1) * P], ident[:])

        def empty_c(n):
            cg = work.tile([P, 1024], BF16, name="cg", bufs=4, align_bytes=64)
            nc.scalar.copy(
                out=cg[:].bitcast(F32).rearrange("p (j n u) -> p j n u", j=2, u=2),
                in_=state["ct", n][:].rearrange("p j u n -> p j n u"),
            )
            state["cg", n] = cg

        def quant_c(n):
            cc = work.tile([P, 256], U32, name="cc", bufs=4, align_bytes=64)
            cs = work.tile([P, 256], U8, name="cs", bufs=4, align_bytes=64)
            nc.vector.quantize_mx(out=cc[:].bitcast(FP8X4), scales=cs[:], in_=state["cg", n][:])
            state["cc", n] = (cc, cs)


        def mm_kv_rope(n):
            cc, cs = state["cc", n]
            xc, xsc = state["xc", n]
            pr = ps_q.tile([P, OUT_W], F32, name="pr", bufs=2)
            for j in range(2):
                cols = slice(j * P, (j + 1) * P)
                for g in range(2):
                    xcols = slice((2 * j + g) * P, (2 * j + g + 1) * P)
                    nc.tensor.matmul_mx(
                        out=pr[:, 384 * j : 384 * j + 128],
                        lhsT=xc[:, xcols].bitcast(FP8X4),
                        lhsT_scale=xsc[:, xcols],
                        rhs=wkv_c[:, j, g, :].bitcast(FP8X4),
                        rhs_scale=wkv_s[:, j, g, :],
                        start=(g == 0),
                        stop=(g == 1),
                    )
                nc.tensor.matmul_mx(
                    out=pr[:, 128 + 128 * j : 256 + 128 * j],
                    lhsT=cc[:, cols].bitcast(FP8X4),
                    lhsT_scale=cs[:, cols],
                    rhs=wb_c[:, 256:384].bitcast(FP8X4),
                    rhs_scale=wb_s[:, 256:384],
                    start=True,
                    stop=True,
                )
            state["pr", n] = pr

        def mm_nope(n):
            cc, cs = state["cc", n]
            pn = ps_q.tile([P, 2, 256], F32, name="pn", bufs=1)
            for j in range(2):
                cols = slice(j * P, (j + 1) * P)
                nc.tensor.matmul_mx(
                    out=pn[:, j, :],
                    lhsT=cc[:, cols].bitcast(FP8X4),
                    lhsT_scale=cs[:, cols],
                    rhs=wb_c[:, 0:256].bitcast(FP8X4),
                    rhs_scale=wb_s[:, 0:256],
                    start=True,
                    stop=True,
                )
            state["pn", n] = pn


        def out_tile(n):
            if ("ot", n) not in state:
                state["ot", n] = work.tile([P, 1152], F32, name="ot", bufs=6)
            return state["ot", n]

        def copy_nope(n):
            nc.scalar.copy(
                out=out_tile(n)[:, 128:896].rearrange("p (h c) -> p h c", c=DN + DR)[:, :, 0:DN],
                in_=state["pn", n][:].rearrange("p j (h c) -> p (j h) c", h=NH),
            )

        def square_kv(n):
            mean = stat("mean", n + KV_LAG)
            for j in range(2):
                squares = work.tile([P, KVR], BF16, name="squares_kv")
                nc.scalar.activation(
                    squares[:],
                    state["pr", n][:, 448 * j : 448 * j + KVR],
                    ACT.Square,
                    scale=KVR**-0.5,
                    accum_out=mean[:, 2 + j : 3 + j],
                )

        def gain_kv(n):
            gained = work.tile([P, 2, KVR], F32, name="gained", bufs=5)
            nc.vector.tensor_tensor(
                out=gained[:],
                in0=state["pr", n][:].rearrange("p (b c) -> p b c", c=KVR)[:, 0:8:7, :],
                in1=gkv[:].unsqueeze(1).to_broadcast([P, 2, KVR]),
                op=MULT,
            )
            state["gained", n] = gained

        def scale_ckv(n):
            for j in range(2):
                nc.scalar.activation(
                    out_tile(n)[:, 960 * j : 960 * j + KVR],
                    state["gained", n][:, j, :],
                    ACT.Copy,
                    scale=stat("rinv", n + KV_LAG)[:, 2 + j : 3 + j],
                )

        def rope_products(n):
            products = work.tile([P, 6, 2, 2, HALF], F32, name="products", bufs=4)
            nc.vector.tensor_tensor(
                out=products[:].rearrange("p (j s) h w d -> p j s h w d", j=2),
                in0=state["pr", n][:, 64:448]
                .rearrange("p (j s h d) -> p j s h d", j=2, s=3, h=2)
                .unsqueeze(4)
                .to_broadcast([P, 2, 3, 2, 2, HALF]),
                in1=factors[:, 2 * n : 2 * n + 2].unsqueeze(2).to_broadcast([P, 2, 3, 2, 2, HALF]),
                op=MULT,
            )
            state["products", n] = products

        def rope_add(n, engine):
            products = state["products", n][:].rearrange("p s h w d -> p s h (w d)")
            engine.tensor_tensor(
                out=out_tile(n)[:].rearrange("p (s c) -> p s c", c=DN + DR)[:, :, 64:128],
                in0=products[:, :, 0, :],
                in1=products[:, :, 1, :],
                op=ADD,
            )

        def store(n):
            ot = out_tile(n)
            nc.sync.dma_start(
                out=out_hbm[:, 2 * n : 2 * n + 2, 0:384], in_=ot[:, 128:896].rearrange("p (j c) -> p j c", j=2)
            )
            nc.sync.dma_start(
                out=out_hbm[:, 2 * n : 2 * n + 2, 384:512],
                in_=ot[:].rearrange("p (b c) -> p b c", c=192)[:, 0:6:5, 0:128],
            )

        OPS = dict(
            mult=(-1, mult_x),
            gate=(-1, gate),
            turn0=(0, lambda n: turn_x(n, 0)),
            turn1=(0, lambda n: turn_x(n, 1)),
            empty0=(0, lambda n: empty_x(n, 0)),
            empty1=(0, lambda n: empty_x(n, 1)),
            quant_x=(1, quant_x),
            a0=(NORM_LAG, lambda n: mm_a(n, 0)),
            a1=(NORM_LAG, lambda n: mm_a(n, 1)),
            square0=(NORM_LAG, lambda n: square_a(n, 0)),
            square1=(NORM_LAG, lambda n: square_a(n, 1)),
            norm0=(NORM_LAG, lambda n: norm_a(n, 0)),
            norm1=(NORM_LAG, lambda n: norm_a(n, 1)),
            turn_c0=(NORM_LAG, lambda n: turn_c(n, 0)),
            turn_c1=(NORM_LAG, lambda n: turn_c(n, 1)),
            empty_c=(NORM_LAG, empty_c),
            quant_c=(3, quant_c),
            kv_rope=(3, mm_kv_rope),
            nope=(3, mm_nope),
            copy=(3, copy_nope),
            rope=(4, rope_products),
            gain=(4, gain_kv),
            square_kv=(4, square_kv),
            add=(5, lambda n: rope_add(n, nc.gpsimd)),
            add_vector=(5, lambda n: rope_add(n, nc.vector)),
            ckv=(KV_LAG, scale_ckv),
            store=(5, store),
            rms=(0, lambda s: inverse_rms(s, 0, 4)),
            rms_a=(0, lambda n: inverse_rms(n + NORM_LAG, 0, 2)),
            rms_kv=(0, lambda n: inverse_rms(n + KV_LAG, 2, 4)),
            wa_scalar=(0, lambda part: wa_copy(nc.scalar.copy, part)),
            wa_vector=(0, lambda part: wa_copy(nc.vector.tensor_copy, part)),
            wa_quant=(0, wa_quant),
            gamma=(0, gamma_copy),
            wb_copy=(0, wb_copy),
            wb_quant=(0, wb_quant),
            table=(0, rope_table),
            dummies=(0, dummies),
        )
        for word in FIRST.split():
            stage, number = word.split(":")
            OPS[stage][1](int(number))
        for s in range(FIRST_STEP, PAIRS - 1):
            for stage in STEP.split():
                lag, run = OPS[stage]
                run(s - lag)
        for word in LAST.split():
            stage, number = word.split(":")
            OPS[stage][1](PAIRS + int(number))
